import numpy as np
import ml_dtypes


def mxq(x, axis, fmt="e4m3"):
    dtype, down = {"e4m3": (ml_dtypes.float8_e4m3fn, 7), "e5m2": (ml_dtypes.float8_e5m2, 14)}[fmt]
    v = np.moveaxis(np.asarray(x, np.float32).astype(ml_dtypes.bfloat16).astype(np.float64), axis, -1)
    blocks = v.reshape(v.shape[:-1] + (-1, 32))
    amax = np.abs(blocks).max(-1, keepdims=True)
    byte = np.maximum(np.where(amax > 0, np.frexp(amax)[1] - 1 + 127, 0) - down, 1)
    scale = np.exp2(byte - 127.0)
    codes = (blocks / scale).astype(np.float32).astype(dtype).astype(np.float64)
    return np.moveaxis((codes * scale).reshape(v.shape), -1, axis)


WIDE = False


def mx_kscale(k):
    if not WIDE:
        return np.ones(k)
    levels = np.array([10, -10, 5, -5, 0])
    a = np.random.permutation(np.resize(levels, k // 512 * 4)).reshape(k // 512, 4)
    idx = np.arange(k)
    return np.exp2(a[idx // 512, idx % 128 // 32])


BF16 = ml_dtypes.bfloat16


def bf(x):
    return np.asarray(x, np.float32).astype(BF16)


def f64(x):
    return np.asarray(x).astype(np.float64)


E2M1 = np.array([0.0, 0.5, 1.0, 1.5, 2.0, 3.0, 4.0, 6.0, -0.0, -0.5, -1.0, -1.5, -2.0, -3.0, -4.0, -6.0])


def pack_weight(w, fmt):
    k, n = w.shape
    w = f64(bf(w)).reshape(k // 32, 32, n)
    amax = np.abs(w).max(1)
    if fmt == "e4m3":
        byte = np.frexp(amax)[1] - 1 + 127 - 7
    else:
        mant, ex = np.frexp(amax / 6.0)
        byte = np.where(mant > 0.5, ex, ex - 1) + 127
    byte = np.clip(np.where(amax > 0, byte, 1), 1, 254)
    scaled = (w * np.exp2(127.0 - byte)[:, None, :]).reshape(k, n).astype(np.float32)
    by_word = np.ascontiguousarray(scaled.reshape(k // 512, 128, 4, n).transpose(0, 1, 3, 2))
    if fmt == "e4m3":
        words = by_word.astype(ml_dtypes.float8_e4m3fn).view(np.uint8)
    else:
        c = by_word.astype(ml_dtypes.float4_e2m1fn).view(np.uint8) & 0xF
        words = c[..., 0::2] | (c[..., 1::2] << 4)
    return np.ascontiguousarray(words), np.ascontiguousarray(byte.astype(np.uint8).reshape(k // 512, 16, n))


def unpack_weight(words, scales, fmt):
    g, p, n, _ = words.shape
    if fmt == "e4m3":
        vals = np.ascontiguousarray(words).view(ml_dtypes.float8_e4m3fn).astype(np.float64)
    else:
        nib = np.empty((g, p, n, 4), np.uint8)
        nib[..., 0::2] = words & 0xF
        nib[..., 1::2] = words >> 4
        vals = E2M1[nib]
    vals = vals * np.repeat(np.exp2(scales.astype(np.float64) - 127.0), 8, axis=1)[..., None]
    return vals.transpose(0, 1, 3, 2).reshape(g * 512, n)


B, T, D, E, F = 4, 1024, 512, 1024, 256
EPS = 1e-6
FMT = "e4m3"


def rms_norm(x, w):
    rms = np.sqrt(np.mean(x * x, axis=-1, keepdims=True) + EPS)
    return x / rms * w


def erf(v):
    a = np.minimum(np.abs(v), 6.0)
    z = 2.0 * a * a
    term = a.copy()
    tot = a.copy()
    for n in range(1, 110):
        term = term * z / (2 * n + 1)
        tot = tot + term
    return np.sign(v) * tot * np.exp(-a * a) * 2.0 / np.sqrt(np.pi)


def gelu_erf(v):
    return 0.5 * v * (1.0 + erf(v / np.sqrt(2.0)))


def setup_inputs():
    s, t = mx_kscale(E), mx_kscale(D)
    attn = bf(np.random.standard_normal((B, T, E)) * 0.6 * s)
    x = bf(np.random.standard_normal((B, T, D)))
    wo_words, wo_scales = pack_weight(np.random.standard_normal((E, D)) / np.sqrt(E) / s[:, None], FMT)
    bo = bf(np.random.standard_normal(D) * 0.1)
    mlp_norm_w = bf((1.0 + 0.1 * np.random.standard_normal(D)) * t)
    w1_words, w1_scales = pack_weight(np.random.standard_normal((D, F)) / np.sqrt(D) / t[:, None], FMT)
    b1 = bf(np.random.standard_normal(F) * 0.1)
    return {"attn": attn,
            "x": x,
            "wo_words": wo_words,
            "wo_scales": wo_scales,
            "bo": bo,
            "mlp_norm_w": mlp_norm_w,
            "w1_words": w1_words,
            "w1_scales": w1_scales,
            "b1": b1}


def reference(attn, x, wo_words, wo_scales, bo, mlp_norm_w, w1_words, w1_scales, b1):
    x_mid = f64(x) + (mxq(f64(attn), 2, "e4m3") @ unpack_weight(wo_words, wo_scales, FMT)) + f64(bo)
    h = rms_norm(x_mid, f64(mlp_norm_w))
    g = gelu_erf((mxq(h, 2, "e4m3") @ unpack_weight(w1_words, w1_scales, FMT)) + f64(b1))
    return x_mid, g

@@ -1,0 +1,277 @@
+import math
+from contextlib import ExitStack
+
+import concourse.mybir as mybir
+from concourse.masks import make_identity
+
+F32 = mybir.dt.float32
+BF16 = mybir.dt.bfloat16
+I32 = mybir.dt.int32
+U32 = mybir.dt.uint32
+U8 = mybir.dt.uint8
+FP8X4 = mybir.dt.float8_e4m3fn_x4
+ACT = mybir.ActivationFunctionType
+ALU = mybir.AluOpType
+
+P = 128
+PACK = 4
+K_PASS = P * PACK
+TOKENS = 4 * 1024
+E = 1024
+D = 512
+F = 256
+EPS = 1e-6
+E_PASSES = E // K_PASS
+N_TILES = TOKENS // P
+CHUNK = 4
+N_CHUNKS = N_TILES // CHUNK
+
+FLOPS = 2 * TOKENS * (E * D + D * F)
+
+
+def tile_tinyblock_pb_t_kernel(
+    tc, attn, x, wo_words, wo_scales, bo, mlp_norm_w, w1_words, w1_scales, b1, out_0, out_1
+):
+    nc = tc.nc
+
+    attn_v = attn.flatten_outer_dims().rearrange("(p i) k -> p i k", i=N_TILES)
+    x_v = x.flatten_outer_dims().rearrange("(p i) d -> p i d", i=N_TILES)
+    x_mid_v = out_0.flatten_outer_dims().rearrange("(p i) d -> p i d", i=N_TILES)
+    g_v = out_1.flatten_outer_dims().rearrange("(p i) f -> p i f", i=N_TILES)
+
+    with ExitStack() as stack:
+        const = stack.enter_context(tc.tile_pool(name="const", bufs=1))
+        loads = stack.enter_context(tc.tile_pool(name="loads", bufs=N_CHUNKS))
+        work = stack.enter_context(tc.tile_pool(name="work", bufs=3))
+        small = stack.enter_context(tc.tile_pool(name="small", bufs=4))
+        stores = stack.enter_context(tc.tile_pool(name="stores", bufs=3))
+        psum = stack.enter_context(tc.psum_pool(name="psum", bufs=2))
+        stack.enter_context(tc.manual_schedule())
+
+        ident = const.tile([P, P], F32)
+        make_identity(nc, ident[:])
+
+        wo_planes = const.tile([P, E_PASSES, D], U8, align_bytes=64)
+        w1_planes = const.tile([P, F], U8, align_bytes=64)
+        nc.vector.memset(wo_planes[:].bitcast(I32), 0)
+        nc.vector.memset(w1_planes[:].bitcast(I32), 0)
+        neg_half = const.tile([P, 1], F32)
+        nc.vector.memset(neg_half[:], -0.5)
+
+        warm_in = const.tile([P, 1], F32)
+        warm_out = const.tile([P, 1], F32)
+        nc.vector.memset(warm_in[:], 0.0)
+        nc.scalar.activation(out=warm_out[:], in_=warm_in[:], func=ACT.Gelu)
+
+        bo_bc = const.tile([P, D], BF16)
+        nc.scalar.dma_start(out=bo_bc[:], in_=bo.partition_broadcast(P))
+        gain = const.tile([P, PACK], BF16)
+        nc.scalar.dma_start(out=gain[:], in_=mlp_norm_w.rearrange("(p t) -> p t", t=PACK))
+        b1_bc = const.tile([P, F], BF16)
+        nc.scalar.dma_start(out=b1_bc[:], in_=b1.partition_broadcast(P))
+
+        attn_sb = {}
+        x_sb = {}
+
+        def load_attn(c):
+            attn_c = loads.tile([P, CHUNK, E], BF16, tag="attn")
+            nc.sync.dma_start(out=attn_c[:], in_=attn_v[:, c * CHUNK : (c + 1) * CHUNK, :])
+            attn_sb[c] = attn_c
+
+        def load_x(c):
+            x_c = loads.tile([P, CHUNK, D], BF16, tag="x")
+            nc.sync.dma_start(out=x_c[:], in_=x_v[:, c * CHUNK : (c + 1) * CHUNK, :])
+            x_sb[c] = x_c
+
+        load_attn(0)
+        for quadrant in range(4):
+            rows = slice(4 * quadrant, 4 * quadrant + 4)
+            nc.sync.dma_start(
+                out=wo_planes[32 * quadrant : 32 * quadrant + 4, :, :].bitcast(I32),
+                in_=wo_scales[:, rows, :].rearrange("g r n -> r g n").bitcast(I32),
+            )
+        wo_sb = const.tile([P, E_PASSES, D * PACK], U8, align_bytes=64)
+        for g in range(E_PASSES):
+            nc.sync.dma_start(
+                out=wo_sb[:, g, :].bitcast(I32),
+                in_=wo_words[g].rearrange("p n t -> p (n t)").bitcast(I32),
+            )
+        load_x(0)
+        load_attn(1)
+        for quadrant in range(4):
+            rows = slice(4 * quadrant, 4 * quadrant + 4)
+            nc.sync.dma_start(
+                out=w1_planes[32 * quadrant : 32 * quadrant + 4, :].bitcast(I32),
+                in_=w1_scales[0, rows, :].bitcast(I32),
+            )
+        w1_sb = const.tile([P, F * PACK], U8, align_bytes=64)
+        nc.sync.dma_start(
+            out=w1_sb[:].bitcast(I32), in_=w1_words[0].rearrange("p n t -> p (n t)").bitcast(I32)
+        )
+        load_x(1)
+        for c in range(2, N_CHUNKS):
+            load_attn(c)
+            load_x(c)
+
+        attn_t_of = {}
+        attn_grouped_of = {}
+        attn_mx_of = {}
+        xb_of = {}
+        x_mid_of = {}
+        rstd_of = {}
+        y_of = {}
+        h_grouped_of = {}
+        h_mx_of = {}
+        pre_gelu_of = {}
+        g_of = {}
+
+        def transpose_attn(i):
+            words = attn_sb[i // CHUNK][:, i % CHUNK, :].bitcast(F32)
+            attn_t = psum.tile([P, E_PASSES, 2, P], F32, tag="attn_t")
+            for g in range(E_PASSES):
+                for u in range(2):
+                    nc.tensor.transpose(
+                        attn_t[:, g, u, :], words[:, 256 * g + u : 256 * (g + 1) : 2], ident[:]
+                    )
+            attn_t_of[i] = attn_t
+
+        def regroup_attn(i):
+            attn_grouped = work.tile([P, E_PASSES, P, PACK], BF16, align_bytes=64)
+            nc.scalar.copy(
+                out=attn_grouped[:].bitcast(F32), in_=attn_t_of[i][:].rearrange("p g u r -> p g r u")
+            )
+            attn_grouped_of[i] = attn_grouped
+
+        def quantise_attn(i):
+            attn_codes = work.tile([P, E_PASSES * P], U32, align_bytes=64)
+            attn_scales = work.tile([P, E_PASSES * P], U8, align_bytes=64)
+            nc.vector.quantize_mx(
+                out=attn_codes[:].bitcast(FP8X4),
+                scales=attn_scales[:],
+                in_=attn_grouped_of[i][:].rearrange("p g r t -> p (g r t)"),
+            )
+            attn_mx_of[i] = (attn_codes, attn_scales)
+
+        def add_bias(i):
+            xb = work.tile([P, D], F32)
+            nc.vector.tensor_tensor(
+                out=xb[:], in0=x_sb[i // CHUNK][:, i % CHUNK, :], in1=bo_bc[:], op=ALU.add
+            )
+            xb_of[i] = xb
+
+        def first_matmul(i):
+            attn_codes, attn_scales = attn_mx_of[i]
+            acc = psum.tile([P, D], F32, tag="acc")
+            for g in range(E_PASSES):
+                cols = slice(g * P, (g + 1) * P)
+                nc.tensor.matmul_mx(
+                    out=acc[:],
+                    lhsT=attn_codes[:, cols].bitcast(FP8X4),
+                    lhsT_scale=attn_scales[:, cols],
+                    rhs=wo_sb[:, g, :].bitcast(FP8X4),
+                    rhs_scale=wo_planes[:, g, :],
+                    start=(g == 0),
+                    stop=(g == E_PASSES - 1),
+                )
+            c = i // CHUNK
+            if i % CHUNK == 0:
+                x_mid_c = stores.tile([P, CHUNK, D], F32, tag="x_mid")
+                x_mid_of[c] = x_mid_c
+            nc.vector.tensor_tensor(
+                out=x_mid_of[c][:, i % CHUNK, :], in0=acc[:], in1=xb_of[i][:], op=ALU.add
+            )
+            if i % CHUNK == CHUNK - 1:
+                nc.sync.dma_start(out=x_mid_v[:, c * CHUNK : (c + 1) * CHUNK, :], in_=x_mid_of[c][:])
+
+        def inverse_rms(i):
+            squares = work.tile([P, D], BF16)
+            mean_sq = small.tile([P, 1], F32)
+            nc.scalar.activation(
+                out=squares[:],
+                in_=x_mid_of[i // CHUNK][:, i % CHUNK, :],
+                func=ACT.Square,
+                scale=1.0 / math.sqrt(D),
+                accum_out=mean_sq[:],
+            )
+            mean_sq_eps = small.tile([P, 1], F32)
+            nc.gpsimd.tensor_scalar(
+                out=mean_sq_eps[:], in0=mean_sq[:], scalar1=1.0, scalar2=EPS, op0=ALU.mult, op1=ALU.add
+            )
+            rstd = small.tile([P, 1], F32)
+            nc.gpsimd.tensor_tensor(out=rstd[:], in0=mean_sq_eps[:], in1=neg_half[:], op=ALU.pow)
+            rstd_of[i] = rstd
+
+        def normalise(i):
+            y = work.tile([P, PACK, P], F32)
+            nc.scalar.activation(
+                out=y[:].rearrange("p t q -> p q t"),
+                in_=x_mid_of[i // CHUNK][:, i % CHUNK, :].rearrange("p (q t) -> p q t", t=PACK),
+                func=ACT.Copy,
+                scale=rstd_of[i][:],
+            )
+            y_of[i] = y
+
+        def transpose_h(i):
+            y_t = psum.tile([P, PACK, P], F32, tag="y_t")
+            for t in range(PACK):
+                nc.tensor.transpose(y_t[:, t, :], y_of[i][:, t, :], ident[:])
+            h_grouped = work.tile([P, P, PACK], BF16, align_bytes=64)
+            nc.vector.tensor_tensor(
+                out=h_grouped[:],
+                in0=y_t[:].rearrange("p t r -> p r t"),
+                in1=gain[:].unsqueeze(1).to_broadcast([P, P, PACK]),
+                op=ALU.mult,
+            )
+            h_grouped_of[i] = h_grouped
+
+        def quantise_h(i):
+            h_codes = work.tile([P, P], U32, align_bytes=64)
+            h_scales = work.tile([P, P], U8, align_bytes=64)
+            nc.vector.quantize_mx(
+                out=h_codes[:].bitcast(FP8X4),
+                scales=h_scales[:],
+                in_=h_grouped_of[i][:].rearrange("p r t -> p (r t)"),
+            )
+            h_mx_of[i] = (h_codes, h_scales)
+
+        def second_matmul(i):
+            h_codes, h_scales = h_mx_of[i]
+            g_acc = psum.tile([P, F], F32, tag="g_acc")
+            nc.tensor.matmul_mx(
+                out=g_acc[:],
+                lhsT=h_codes[:].bitcast(FP8X4),
+                lhsT_scale=h_scales[:],
+                rhs=w1_sb[:].bitcast(FP8X4),
+                rhs_scale=w1_planes[:],
+                start=True,
+                stop=True,
+            )
+            pre_gelu = work.tile([P, F], F32)
+            nc.vector.tensor_tensor(out=pre_gelu[:], in0=g_acc[:], in1=b1_bc[:], op=ALU.add)
+            pre_gelu_of[i] = pre_gelu
+
+        def gelu(i):
+            c = i // CHUNK
+            if i % CHUNK == 0:
+                g_c = stores.tile([P, CHUNK, F], F32, tag="g")
+                g_of[c] = g_c
+            nc.scalar.activation(out=g_of[c][:, i % CHUNK, :], in_=pre_gelu_of[i][:], func=ACT.Gelu)
+            if i % CHUNK == CHUNK - 1:
+                nc.sync.dma_start(out=g_v[:, c * CHUNK : (c + 1) * CHUNK, :], in_=g_of[c][:])
+
+        def run(stage, i):
+            if 0 <= i < N_TILES:
+                stage(i)
+
+        for k in range(-3, N_TILES + 5):
+            run(first_matmul, k)
+            run(second_matmul, k - 5)
+            run(transpose_h, k - 3)
+            run(transpose_attn, k + 3)
+            run(regroup_attn, k + 2)
+            run(inverse_rms, k)
+            run(gelu, k - 5)
+            run(normalise, k - 1)
+            run(quantise_attn, k + 2)
+            run(quantise_h, k - 3)
+            run(add_bias, k + 1)

@@ -23,6 +23,7 @@ F = 256
 EPS = 1e-6
 E_PASSES = E // K_PASS
 N_TILES = TOKENS // P
+PAIR = 2
 CHUNK = 4
 N_CHUNKS = N_TILES // CHUNK
 
@@ -55,7 +56,7 @@ def tile_tinyblock_pb_t_kernel(
         w1_planes = const.tile([P, F], U8, align_bytes=64)
         nc.vector.memset(wo_planes[:].bitcast(I32), 0)
         nc.vector.memset(w1_planes[:].bitcast(I32), 0)
-        neg_half = const.tile([P, 1], F32)
+        neg_half = const.tile([P, PAIR], F32)
         nc.vector.memset(neg_half[:], -0.5)
 
         warm_in = const.tile([P, 1], F32)
@@ -118,10 +119,12 @@ def tile_tinyblock_pb_t_kernel(
         attn_mx_of = {}
         xb_of = {}
         x_mid_of = {}
+        mean_sq_of = {}
         rstd_of = {}
         y_of = {}
         h_grouped_of = {}
         h_mx_of = {}
+        g_acc_of = {}
         pre_gelu_of = {}
         g_of = {}
 
@@ -136,38 +139,43 @@ def tile_tinyblock_pb_t_kernel(
             attn_t_of[i] = attn_t
 
         def regroup_attn(i):
-            attn_grouped = work.tile([P, E_PASSES, P, PACK], BF16, align_bytes=64)
+            if i % PAIR == 0:
+                attn_grouped = work.tile([P, PAIR, E_PASSES, P, PACK], BF16, align_bytes=64)
+                attn_grouped_of[i // PAIR] = attn_grouped
             nc.scalar.copy(
-                out=attn_grouped[:].bitcast(F32), in_=attn_t_of[i][:].rearrange("p g u r -> p g r u")
+                out=attn_grouped_of[i // PAIR][:, i % PAIR, :, :, :].bitcast(F32),
+                in_=attn_t_of[i][:].rearrange("p g u r -> p g r u"),
             )
-            attn_grouped_of[i] = attn_grouped
 
-        def quantise_attn(i):
-            attn_codes = work.tile([P, E_PASSES * P], U32, align_bytes=64)
-            attn_scales = work.tile([P, E_PASSES * P], U8, align_bytes=64)
+        def quantise_attn(m):
+            attn_codes = work.tile([P, PAIR, E_PASSES, P], U32, align_bytes=64)
+            attn_scales = work.tile([P, PAIR, E_PASSES, P], U8, align_bytes=64)
             nc.vector.quantize_mx(
-                out=attn_codes[:].bitcast(FP8X4),
-                scales=attn_scales[:],
-                in_=attn_grouped_of[i][:].rearrange("p g r t -> p (g r t)"),
+                out=attn_codes[:].rearrange("p i g r -> p (i g r)").bitcast(FP8X4),
+                scales=attn_scales[:].rearrange("p i g r -> p (i g r)"),
+                in_=attn_grouped_of[m][:].rearrange("p i g r t -> p (i g r t)"),
             )
-            attn_mx_of[i] = (attn_codes, attn_scales)
+            attn_mx_of[m] = (attn_codes, attn_scales)
 
-        def add_bias(i):
-            xb = work.tile([P, D], F32)
+        def add_bias(m):
+            first = m * PAIR
+            xb = work.tile([P, PAIR, D], F32)
             nc.vector.tensor_tensor(
-                out=xb[:], in0=x_sb[i // CHUNK][:, i % CHUNK, :], in1=bo_bc[:], op=ALU.add
+                out=xb[:],
+                in0=x_sb[first // CHUNK][:, first % CHUNK : first % CHUNK + PAIR, :],
+                in1=bo_bc[:].unsqueeze(1).to_broadcast([P, PAIR, D]),
+                op=ALU.add,
             )
-            xb_of[i] = xb
+            xb_of[m] = xb
 
         def first_matmul(i):
-            attn_codes, attn_scales = attn_mx_of[i]
+            attn_codes, attn_scales = attn_mx_of[i // PAIR]
             acc = psum.tile([P, D], F32, tag="acc")
             for g in range(E_PASSES):
-                cols = slice(g * P, (g + 1) * P)
                 nc.tensor.matmul_mx(
                     out=acc[:],
-                    lhsT=attn_codes[:, cols].bitcast(FP8X4),
-                    lhsT_scale=attn_scales[:, cols],
+                    lhsT=attn_codes[:, i % PAIR, g, :].bitcast(FP8X4),
+                    lhsT_scale=attn_scales[:, i % PAIR, g, :],
                     rhs=wo_sb[:, g, :].bitcast(FP8X4),
                     rhs_scale=wo_planes[:, g, :],
                     start=(g == 0),
@@ -178,28 +186,32 @@ def tile_tinyblock_pb_t_kernel(
                 x_mid_c = stores.tile([P, CHUNK, D], F32, tag="x_mid")
                 x_mid_of[c] = x_mid_c
             nc.vector.tensor_tensor(
-                out=x_mid_of[c][:, i % CHUNK, :], in0=acc[:], in1=xb_of[i][:], op=ALU.add
+                out=x_mid_of[c][:, i % CHUNK, :], in0=acc[:], in1=xb_of[i // PAIR][:, i % PAIR, :], op=ALU.add
             )
             if i % CHUNK == CHUNK - 1:
                 nc.sync.dma_start(out=x_mid_v[:, c * CHUNK : (c + 1) * CHUNK, :], in_=x_mid_of[c][:])
 
-        def inverse_rms(i):
+        def mean_of_squares(i):
+            if i % PAIR == 0:
+                mean_sq = small.tile([P, PAIR], F32)
+                mean_sq_of[i // PAIR] = mean_sq
             squares = work.tile([P, D], BF16)
-            mean_sq = small.tile([P, 1], F32)
             nc.scalar.activation(
                 out=squares[:],
                 in_=x_mid_of[i // CHUNK][:, i % CHUNK, :],
                 func=ACT.Square,
                 scale=1.0 / math.sqrt(D),
-                accum_out=mean_sq[:],
+                accum_out=mean_sq_of[i // PAIR][:, i % PAIR : i % PAIR + 1],
             )
-            mean_sq_eps = small.tile([P, 1], F32)
+
+        def inverse_rms(m):
+            mean_sq_eps = small.tile([P, PAIR], F32)
             nc.gpsimd.tensor_scalar(
-                out=mean_sq_eps[:], in0=mean_sq[:], scalar1=1.0, scalar2=EPS, op0=ALU.mult, op1=ALU.add
+                out=mean_sq_eps[:], in0=mean_sq_of[m][:], scalar1=1.0, scalar2=EPS, op0=ALU.mult, op1=ALU.add
             )
-            rstd = small.tile([P, 1], F32)
+            rstd = small.tile([P, PAIR], F32)
             nc.gpsimd.tensor_tensor(out=rstd[:], in0=mean_sq_eps[:], in1=neg_half[:], op=ALU.pow)
-            rstd_of[i] = rstd
+            rstd_of[m] = rstd
 
         def normalise(i):
             y = work.tile([P, PACK, P], F32)
@@ -207,7 +219,7 @@ def tile_tinyblock_pb_t_kernel(
                 out=y[:].rearrange("p t q -> p q t"),
                 in_=x_mid_of[i // CHUNK][:, i % CHUNK, :].rearrange("p (q t) -> p q t", t=PACK),
                 func=ACT.Copy,
-                scale=rstd_of[i][:],
+                scale=rstd_of[i // PAIR][:, i % PAIR : i % PAIR + 1],
             )
             y_of[i] = y
 
@@ -215,63 +227,82 @@ def tile_tinyblock_pb_t_kernel(
             y_t = psum.tile([P, PACK, P], F32, tag="y_t")
             for t in range(PACK):
                 nc.tensor.transpose(y_t[:, t, :], y_of[i][:, t, :], ident[:])
-            h_grouped = work.tile([P, P, PACK], BF16, align_bytes=64)
+            if i % PAIR == 0:
+                h_grouped = work.tile([P, PAIR, P, PACK], BF16, align_bytes=64)
+                h_grouped_of[i // PAIR] = h_grouped
             nc.vector.tensor_tensor(
-                out=h_grouped[:],
+                out=h_grouped_of[i // PAIR][:, i % PAIR, :, :],
                 in0=y_t[:].rearrange("p t r -> p r t"),
                 in1=gain[:].unsqueeze(1).to_broadcast([P, P, PACK]),
                 op=ALU.mult,
             )
-            h_grouped_of[i] = h_grouped
 
-        def quantise_h(i):
-            h_codes = work.tile([P, P], U32, align_bytes=64)
-            h_scales = work.tile([P, P], U8, align_bytes=64)
+        def quantise_h(m):
+            h_codes = work.tile([P, PAIR, P], U32, align_bytes=64)
+            h_scales = work.tile([P, PAIR, P], U8, align_bytes=64)
             nc.vector.quantize_mx(
-                out=h_codes[:].bitcast(FP8X4),
-                scales=h_scales[:],
-                in_=h_grouped_of[i][:].rearrange("p r t -> p (r t)"),
+                out=h_codes[:].rearrange("p i r -> p (i r)").bitcast(FP8X4),
+                scales=h_scales[:].rearrange("p i r -> p (i r)"),
+                in_=h_grouped_of[m][:].rearrange("p i r t -> p (i r t)"),
             )
-            h_mx_of[i] = (h_codes, h_scales)
+            h_mx_of[m] = (h_codes, h_scales)
 
         def second_matmul(i):
-            h_codes, h_scales = h_mx_of[i]
-            g_acc = psum.tile([P, F], F32, tag="g_acc")
+            h_codes, h_scales = h_mx_of[i // PAIR]
+            if i % PAIR == 0:
+                g_acc = psum.tile([P, PAIR, F], F32, tag="g_acc")
+                g_acc_of[i // PAIR] = g_acc
             nc.tensor.matmul_mx(
-                out=g_acc[:],
-                lhsT=h_codes[:].bitcast(FP8X4),
-                lhsT_scale=h_scales[:],
+                out=g_acc_of[i // PAIR][:, i % PAIR, :],
+                lhsT=h_codes[:, i % PAIR, :].bitcast(FP8X4),
+                lhsT_scale=h_scales[:, i % PAIR, :],
                 rhs=w1_sb[:].bitcast(FP8X4),
                 rhs_scale=w1_planes[:],
                 start=True,
                 stop=True,
             )
-            pre_gelu = work.tile([P, F], F32)
-            nc.vector.tensor_tensor(out=pre_gelu[:], in0=g_acc[:], in1=b1_bc[:], op=ALU.add)
-            pre_gelu_of[i] = pre_gelu
 
-        def gelu(i):
-            c = i // CHUNK
-            if i % CHUNK == 0:
+        def add_b1(m):
+            pre_gelu = work.tile([P, PAIR, F], F32)
+            nc.vector.tensor_tensor(
+                out=pre_gelu[:],
+                in0=g_acc_of[m][:],
+                in1=b1_bc[:].unsqueeze(1).to_broadcast([P, PAIR, F]),
+                op=ALU.add,
+            )
+            pre_gelu_of[m] = pre_gelu
+
+        def gelu(m):
+            first = m * PAIR
+            c = first // CHUNK
+            if first % CHUNK == 0:
                 g_c = stores.tile([P, CHUNK, F], F32, tag="g")
                 g_of[c] = g_c
-            nc.scalar.activation(out=g_of[c][:, i % CHUNK, :], in_=pre_gelu_of[i][:], func=ACT.Gelu)
-            if i % CHUNK == CHUNK - 1:
+            nc.scalar.activation(
+                out=g_of[c][:, first % CHUNK : first % CHUNK + PAIR, :], in_=pre_gelu_of[m][:], func=ACT.Gelu
+            )
+            if first % CHUNK == CHUNK - PAIR:
                 nc.sync.dma_start(out=g_v[:, c * CHUNK : (c + 1) * CHUNK, :], in_=g_of[c][:])
 
         def run(stage, i):
             if 0 <= i < N_TILES:
                 stage(i)
 
-        for k in range(-3, N_TILES + 5):
+        def run_pair(stage, i):
+            if 0 <= i < N_TILES and i % PAIR == PAIR - 1:
+                stage(i // PAIR)
+
+        for k in range(-5, N_TILES + 8):
             run(first_matmul, k)
-            run(second_matmul, k - 5)
-            run(transpose_h, k - 3)
-            run(transpose_attn, k + 3)
-            run(regroup_attn, k + 2)
-            run(inverse_rms, k)
-            run(gelu, k - 5)
-            run(normalise, k - 1)
-            run(quantise_attn, k + 2)
-            run(quantise_h, k - 3)
-            run(add_bias, k + 1)
+            run(second_matmul, k - 6)
+            run_pair(add_b1, k - 7)
+            run(transpose_h, k - 4)
+            run(transpose_attn, k + 5)
+            run(regroup_attn, k + 4)
+            run(mean_of_squares, k)
+            run_pair(inverse_rms, k)
+            run_pair(gelu, k - 8)
+            run(normalise, k - 2)
+            run_pair(quantise_attn, k + 3)
+            run_pair(quantise_h, k - 4)
+            run_pair(add_bias, k + 3)

@@ -44,6 +44,7 @@ def tile_tinyblock_pb_t_kernel(
         const = stack.enter_context(tc.tile_pool(name="const", bufs=1))
         loads = stack.enter_context(tc.tile_pool(name="loads", bufs=N_CHUNKS))
         work = stack.enter_context(tc.tile_pool(name="work", bufs=3))
+        ahead = stack.enter_context(tc.tile_pool(name="ahead", bufs=4))
         small = stack.enter_context(tc.tile_pool(name="small", bufs=4))
         stores = stack.enter_context(tc.tile_pool(name="stores", bufs=3))
         psum = stack.enter_context(tc.psum_pool(name="psum", bufs=2))
@@ -159,8 +160,8 @@ def tile_tinyblock_pb_t_kernel(
 
         def add_bias(m):
             first = m * PAIR
-            xb = work.tile([P, PAIR, D], F32)
-            nc.vector.tensor_tensor(
+            xb = ahead.tile([P, PAIR, D], F32)
+            nc.gpsimd.tensor_tensor(
                 out=xb[:],
                 in0=x_sb[first // CHUNK][:, first % CHUNK : first % CHUNK + PAIR, :],
                 in1=bo_bc[:].unsqueeze(1).to_broadcast([P, PAIR, D]),
@@ -301,8 +302,8 @@ def tile_tinyblock_pb_t_kernel(
             run(regroup_attn, k + 4)
             run(mean_of_squares, k)
             run_pair(inverse_rms, k)
+            run_pair(add_bias, k + 5)
             run_pair(gelu, k - 8)
             run(normalise, k - 2)
             run_pair(quantise_attn, k + 3)
             run_pair(quantise_h, k - 4)
-            run_pair(add_bias, k + 3)

@@ -172,16 +172,17 @@ def tile_tinyblock_pb_t_kernel(
         def first_matmul(i):
             attn_codes, attn_scales = attn_mx_of[i // PAIR]
             acc = psum.tile([P, D], F32, tag="acc")
-            for g in range(E_PASSES):
-                nc.tensor.matmul_mx(
-                    out=acc[:],
-                    lhsT=attn_codes[:, i % PAIR, g, :].bitcast(FP8X4),
-                    lhsT_scale=attn_scales[:, i % PAIR, g, :],
-                    rhs=wo_sb[:, g, :].bitcast(FP8X4),
-                    rhs_scale=wo_planes[:, g, :],
-                    start=(g == 0),
-                    stop=(g == E_PASSES - 1),
-                )
+            for repeat in range(2):
+                for g in range(E_PASSES):
+                    nc.tensor.matmul_mx(
+                        out=acc[:],
+                        lhsT=attn_codes[:, i % PAIR, g, :].bitcast(FP8X4),
+                        lhsT_scale=attn_scales[:, i % PAIR, g, :],
+                        rhs=wo_sb[:, g, :].bitcast(FP8X4),
+                        rhs_scale=wo_planes[:, g, :],
+                        start=(g == 0),
+                        stop=(g == E_PASSES - 1),
+                    )
             c = i // CHUNK
             if i % CHUNK == 0:
                 x_mid_c = stores.tile([P, CHUNK, D], F32, tag="x_mid")

@@ -44,7 +44,6 @@ def tile_tinyblock_pb_t_kernel(
         const = stack.enter_context(tc.tile_pool(name="const", bufs=1))
         loads = stack.enter_context(tc.tile_pool(name="loads", bufs=N_CHUNKS))
         work = stack.enter_context(tc.tile_pool(name="work", bufs=3))
-        ahead = stack.enter_context(tc.tile_pool(name="ahead", bufs=4))
         small = stack.enter_context(tc.tile_pool(name="small", bufs=4))
         stores = stack.enter_context(tc.tile_pool(name="stores", bufs=3))
         psum = stack.enter_context(tc.psum_pool(name="psum", bufs=2))
@@ -160,8 +159,8 @@ def tile_tinyblock_pb_t_kernel(
 
         def add_bias(m):
             first = m * PAIR
-            xb = ahead.tile([P, PAIR, D], F32)
-            nc.gpsimd.tensor_tensor(
+            xb = work.tile([P, PAIR, D], F32)
+            nc.vector.tensor_tensor(
                 out=xb[:],
                 in0=x_sb[first // CHUNK][:, first % CHUNK : first % CHUNK + PAIR, :],
                 in1=bo_bc[:].unsqueeze(1).to_broadcast([P, PAIR, D]),
@@ -172,17 +171,16 @@ def tile_tinyblock_pb_t_kernel(
         def first_matmul(i):
             attn_codes, attn_scales = attn_mx_of[i // PAIR]
             acc = psum.tile([P, D], F32, tag="acc")
-            for repeat in range(2):
-                for g in range(E_PASSES):
-                    nc.tensor.matmul_mx(
-                        out=acc[:],
-                        lhsT=attn_codes[:, i % PAIR, g, :].bitcast(FP8X4),
-                        lhsT_scale=attn_scales[:, i % PAIR, g, :],
-                        rhs=wo_sb[:, g, :].bitcast(FP8X4),
-                        rhs_scale=wo_planes[:, g, :],
-                        start=(g == 0),
-                        stop=(g == E_PASSES - 1),
-                    )
+            for g in range(E_PASSES):
+                nc.tensor.matmul_mx(
+                    out=acc[:],
+                    lhsT=attn_codes[:, i % PAIR, g, :].bitcast(FP8X4),
+                    lhsT_scale=attn_scales[:, i % PAIR, g, :],
+                    rhs=wo_sb[:, g, :].bitcast(FP8X4),
+                    rhs_scale=wo_planes[:, g, :],
+                    start=(g == 0),
+                    stop=(g == E_PASSES - 1),
+                )
             c = i // CHUNK
             if i % CHUNK == 0:
                 x_mid_c = stores.tile([P, CHUNK, D], F32, tag="x_mid")
@@ -294,17 +292,17 @@ def tile_tinyblock_pb_t_kernel(
             if 0 <= i < N_TILES and i % PAIR == PAIR - 1:
                 stage(i // PAIR)
 
-        for k in range(-5, N_TILES + 8):
+        for k in range(-5, N_TILES + 11):
             run(first_matmul, k)
-            run(second_matmul, k - 6)
-            run_pair(add_b1, k - 7)
-            run(transpose_h, k - 4)
+            run(second_matmul, k - 9)
+            run_pair(add_b1, k - 10)
+            run(transpose_h, k - 7)
             run(transpose_attn, k + 5)
             run(regroup_attn, k + 4)
             run(mean_of_squares, k)
             run_pair(inverse_rms, k)
-            run_pair(add_bias, k + 5)
-            run_pair(gelu, k - 8)
-            run(normalise, k - 2)
+            run_pair(gelu, k - 11)
+            run(normalise, k - 5)
             run_pair(quantise_attn, k + 3)
-            run_pair(quantise_h, k - 4)
+            run_pair(quantise_h, k - 7)
+            run_pair(add_bias, k + 3)

@@ -66,8 +66,8 @@ def tile_tinyblock_pb_t_kernel(
 
         bo_bc = const.tile([P, D], BF16)
         nc.scalar.dma_start(out=bo_bc[:], in_=bo.partition_broadcast(P))
-        gain = const.tile([P, PACK], BF16)
-        nc.scalar.dma_start(out=gain[:], in_=mlp_norm_w.rearrange("(p t) -> p t", t=PACK))
+        gain_bc = const.tile([P, D], BF16)
+        nc.scalar.dma_start(out=gain_bc[:], in_=mlp_norm_w.partition_broadcast(P))
         b1_bc = const.tile([P, F], BF16)
         nc.scalar.dma_start(out=b1_bc[:], in_=b1.partition_broadcast(P))
 
@@ -121,7 +121,8 @@ def tile_tinyblock_pb_t_kernel(
         x_mid_of = {}
         mean_sq_of = {}
         rstd_of = {}
-        y_of = {}
+        h_of = {}
+        h_t_of = {}
         h_grouped_of = {}
         h_mx_of = {}
         g_acc_of = {}
@@ -214,28 +215,32 @@ def tile_tinyblock_pb_t_kernel(
             rstd_of[m] = rstd
 
         def normalise(i):
-            y = work.tile([P, PACK, P], F32)
-            nc.scalar.activation(
-                out=y[:].rearrange("p t q -> p q t"),
-                in_=x_mid_of[i // CHUNK][:, i % CHUNK, :].rearrange("p (q t) -> p q t", t=PACK),
-                func=ACT.Copy,
-                scale=rstd_of[i // PAIR][:, i % PAIR : i % PAIR + 1],
+            h = work.tile([P, D], BF16)
+            nc.vector.scalar_tensor_tensor(
+                out=h[:],
+                in0=x_mid_of[i // CHUNK][:, i % CHUNK, :],
+                scalar=rstd_of[i // PAIR][:, i % PAIR : i % PAIR + 1],
+                in1=gain_bc[:],
+                op0=ALU.mult,
+                op1=ALU.mult,
             )
-            y_of[i] = y
+            h_of[i] = h
 
         def transpose_h(i):
-            y_t = psum.tile([P, PACK, P], F32, tag="y_t")
-            for t in range(PACK):
-                nc.tensor.transpose(y_t[:, t, :], y_of[i][:, t, :], ident[:])
             if i % PAIR == 0:
-                h_grouped = work.tile([P, PAIR, P, PACK], BF16, align_bytes=64)
-                h_grouped_of[i // PAIR] = h_grouped
-            nc.vector.tensor_tensor(
-                out=h_grouped_of[i // PAIR][:, i % PAIR, :, :],
-                in0=y_t[:].rearrange("p t r -> p r t"),
-                in1=gain[:].unsqueeze(1).to_broadcast([P, P, PACK]),
-                op=ALU.mult,
+                h_t = psum.tile([P, PAIR, 2, P], F32, tag="h_t")
+                h_t_of[i // PAIR] = h_t
+            words = h_of[i][:].bitcast(F32)
+            for u in range(2):
+                nc.tensor.transpose(h_t_of[i // PAIR][:, i % PAIR, u, :], words[:, u::2], ident[:])
+
+        def regroup_h(m):
+            h_grouped = work.tile([P, PAIR, P, PACK], BF16, align_bytes=64)
+            nc.scalar.copy(
+                out=h_grouped[:].bitcast(F32),
+                in_=h_t_of[m][:].rearrange("p i u r -> p i r u"),
             )
+            h_grouped_of[m] = h_grouped
 
         def quantise_h(m):
             h_codes = work.tile([P, PAIR, P], U32, align_bytes=64)
@@ -292,17 +297,18 @@ def tile_tinyblock_pb_t_kernel(
             if 0 <= i < N_TILES and i % PAIR == PAIR - 1:
                 stage(i // PAIR)
 
-        for k in range(-5, N_TILES + 11):
+        for k in range(-5, N_TILES + 14):
             run(first_matmul, k)
-            run(second_matmul, k - 9)
-            run_pair(add_b1, k - 10)
+            run(second_matmul, k - 11)
+            run_pair(add_b1, k - 12)
+            run(normalise, k - 5)
             run(transpose_h, k - 7)
             run(transpose_attn, k + 5)
             run(regroup_attn, k + 4)
             run(mean_of_squares, k)
             run_pair(inverse_rms, k)
-            run_pair(gelu, k - 11)
-            run(normalise, k - 5)
+            run_pair(gelu, k - 13)
+            run_pair(regroup_h, k - 8)
             run_pair(quantise_attn, k + 3)
-            run_pair(quantise_h, k - 7)
+            run_pair(quantise_h, k - 9)
             run_pair(add_bias, k + 3)

@@ -47,6 +47,7 @@ def tile_tinyblock_pb_t_kernel(
         small = stack.enter_context(tc.tile_pool(name="small", bufs=4))
         stores = stack.enter_context(tc.tile_pool(name="stores", bufs=3))
         psum = stack.enter_context(tc.psum_pool(name="psum", bufs=2))
+        psum_one = stack.enter_context(tc.psum_pool(name="psum_one", bufs=1))
         stack.enter_context(tc.manual_schedule())
 
         ident = const.tile([P, P], F32)
@@ -68,8 +69,11 @@ def tile_tinyblock_pb_t_kernel(
         nc.scalar.dma_start(out=bo_bc[:], in_=bo.partition_broadcast(P))
         gain_bc = const.tile([P, D], BF16)
         nc.scalar.dma_start(out=gain_bc[:], in_=mlp_norm_w.partition_broadcast(P))
-        b1_bc = const.tile([P, F], BF16)
-        nc.scalar.dma_start(out=b1_bc[:], in_=b1.partition_broadcast(P))
+        b1_lo = const.tile([P, 1], BF16)
+        nc.scalar.dma_start(out=b1_lo[:], in_=b1[0:P].rearrange("(p o) -> p o", o=1))
+        b1_hi = const.tile([P, 1], BF16)
+        nc.scalar.dma_start(out=b1_hi[:], in_=b1[P : 2 * P].rearrange("(p o) -> p o", o=1))
+        b1_half = [b1_lo, b1_hi]
 
         attn_sb = {}
         x_sb = {}
@@ -125,8 +129,9 @@ def tile_tinyblock_pb_t_kernel(
         h_t_of = {}
         h_grouped_of = {}
         h_mx_of = {}
-        g_acc_of = {}
-        pre_gelu_of = {}
+        g_t_acc_of = {}
+        g_t_of = {}
+        g_back_of = {}
         g_of = {}
 
         def transpose_attn(i):
@@ -252,40 +257,45 @@ def tile_tinyblock_pb_t_kernel(
             )
             h_mx_of[m] = (h_codes, h_scales)
 
-        def second_matmul(i):
-            h_codes, h_scales = h_mx_of[i // PAIR]
-            if i % PAIR == 0:
-                g_acc = psum.tile([P, PAIR, F], F32, tag="g_acc")
-                g_acc_of[i // PAIR] = g_acc
-            nc.tensor.matmul_mx(
-                out=g_acc_of[i // PAIR][:, i % PAIR, :],
-                lhsT=h_codes[:, i % PAIR, :].bitcast(FP8X4),
-                lhsT_scale=h_scales[:, i % PAIR, :],
-                rhs=w1_sb[:].bitcast(FP8X4),
-                rhs_scale=w1_planes[:],
-                start=True,
-                stop=True,
-            )
-
-        def add_b1(m):
-            pre_gelu = work.tile([P, PAIR, F], F32)
-            nc.vector.tensor_tensor(
-                out=pre_gelu[:],
-                in0=g_acc_of[m][:],
-                in1=b1_bc[:].unsqueeze(1).to_broadcast([P, PAIR, F]),
-                op=ALU.add,
-            )
-            pre_gelu_of[m] = pre_gelu
+        def second_matmul(m):
+            h_codes, h_scales = h_mx_of[m]
+            g_t_acc = psum_one.tile([P, 2, PAIR * P], F32, tag="g_t_acc")
+            for j in range(2):
+                nc.tensor.matmul_mx(
+                    out=g_t_acc[:, j, :],
+                    lhsT=w1_sb[:, j * P * PACK : (j + 1) * P * PACK].bitcast(FP8X4),
+                    lhsT_scale=w1_planes[:, j * P : (j + 1) * P],
+                    rhs=h_codes[:].rearrange("p i r -> p (i r)").bitcast(FP8X4),
+                    rhs_scale=h_scales[:].rearrange("p i r -> p (i r)"),
+                    start=True,
+                    stop=True,
+                )
+            g_t_acc_of[m] = g_t_acc
 
         def gelu(m):
+            g_t = work.tile([P, 2, PAIR * P], F32)
+            for j in range(2):
+                nc.scalar.activation(
+                    out=g_t[:, j, :], in_=g_t_acc_of[m][:, j, :], func=ACT.Gelu, bias=b1_half[j][:]
+                )
+            g_t_of[m] = g_t
+
+        def transpose_g(m):
+            g_back = psum_one.tile([P, PAIR, F], F32, tag="g_back")
+            for i in range(PAIR):
+                for j in range(2):
+                    nc.tensor.transpose(
+                        g_back[:, i, j * P : (j + 1) * P], g_t_of[m][:, j, i * P : (i + 1) * P], ident[:]
+                    )
+            g_back_of[m] = g_back
+
+        def store_g(m):
             first = m * PAIR
             c = first // CHUNK
             if first % CHUNK == 0:
                 g_c = stores.tile([P, CHUNK, F], F32, tag="g")
                 g_of[c] = g_c
-            nc.scalar.activation(
-                out=g_of[c][:, first % CHUNK : first % CHUNK + PAIR, :], in_=pre_gelu_of[m][:], func=ACT.Gelu
-            )
+            nc.scalar.copy(out=g_of[c][:, first % CHUNK : first % CHUNK + PAIR, :], in_=g_back_of[m][:])
             if first % CHUNK == CHUNK - PAIR:
                 nc.sync.dma_start(out=g_v[:, c * CHUNK : (c + 1) * CHUNK, :], in_=g_of[c][:])
 
@@ -297,18 +307,19 @@ def tile_tinyblock_pb_t_kernel(
             if 0 <= i < N_TILES and i % PAIR == PAIR - 1:
                 stage(i // PAIR)
 
-        for k in range(-5, N_TILES + 14):
+        for k in range(-5, N_TILES + 13):
             run(first_matmul, k)
-            run(second_matmul, k - 11)
-            run_pair(add_b1, k - 12)
+            run_pair(second_matmul, k - 10)
             run(normalise, k - 5)
+            run_pair(transpose_g, k - 12)
             run(transpose_h, k - 7)
             run(transpose_attn, k + 5)
             run(regroup_attn, k + 4)
+            run_pair(gelu, k - 11)
+            run_pair(store_g, k - 13)
+            run_pair(regroup_h, k - 8)
             run(mean_of_squares, k)
             run_pair(inverse_rms, k)
-            run_pair(gelu, k - 13)
-            run_pair(regroup_h, k - 8)
             run_pair(quantise_attn, k + 3)
             run_pair(quantise_h, k - 9)
-            run_pair(add_bias, k + 3)
+            run_pair(add_bias, k + 4)

@@ -26,6 +26,9 @@ N_TILES = TOKENS // P
 PAIR = 2
 CHUNK = 4
 N_CHUNKS = N_TILES // CHUNK
+N_PAIRS = N_TILES // PAIR
+X_LEAD = 8
+START = -1
 
 FLOPS = 2 * TOKENS * (E * D + D * F)
 
@@ -46,15 +49,15 @@ def tile_tinyblock_pb_t_kernel(
         work = stack.enter_context(tc.tile_pool(name="work", bufs=3))
         small = stack.enter_context(tc.tile_pool(name="small", bufs=4))
         stores = stack.enter_context(tc.tile_pool(name="stores", bufs=3))
+        ahead = stack.enter_context(tc.tile_pool(name="ahead", bufs=X_LEAD // PAIR + 2))
         psum = stack.enter_context(tc.psum_pool(name="psum", bufs=2))
         psum_one = stack.enter_context(tc.psum_pool(name="psum_one", bufs=1))
-        stack.enter_context(tc.manual_schedule())
 
         ident = const.tile([P, P], F32)
         make_identity(nc, ident[:])
 
         wo_planes = const.tile([P, E_PASSES, D], U8, align_bytes=64)
-        w1_planes = const.tile([P, F], U8, align_bytes=64)
+        w1_planes = const.tile([P, 1, F], U8, align_bytes=64)
         nc.vector.memset(wo_planes[:].bitcast(I32), 0)
         nc.vector.memset(w1_planes[:].bitcast(I32), 0)
         neg_half = const.tile([P, PAIR], F32)
@@ -78,45 +81,55 @@ def tile_tinyblock_pb_t_kernel(
         attn_sb = {}
         x_sb = {}
 
-        def load_attn(c):
+        def load_attn(c, pieces):
             attn_c = loads.tile([P, CHUNK, E], BF16, tag="attn")
-            nc.sync.dma_start(out=attn_c[:], in_=attn_v[:, c * CHUNK : (c + 1) * CHUNK, :])
+            tiles = CHUNK // pieces
+            for first in range(0, CHUNK, tiles):
+                nc.sync.dma_start(
+                    out=attn_c[:, first : first + tiles, :],
+                    in_=attn_v[:, c * CHUNK + first : c * CHUNK + first + tiles, :],
+                )
             attn_sb[c] = attn_c
 
-        def load_x(c):
+        def load_x(c, pieces):
             x_c = loads.tile([P, CHUNK, D], BF16, tag="x")
-            nc.sync.dma_start(out=x_c[:], in_=x_v[:, c * CHUNK : (c + 1) * CHUNK, :])
+            tiles = CHUNK // pieces
+            for first in range(0, CHUNK, tiles):
+                nc.sync.dma_start(
+                    out=x_c[:, first : first + tiles, :],
+                    in_=x_v[:, c * CHUNK + first : c * CHUNK + first + tiles, :],
+                )
             x_sb[c] = x_c
 
-        load_attn(0)
-        for quadrant in range(4):
-            rows = slice(4 * quadrant, 4 * quadrant + 4)
-            nc.sync.dma_start(
-                out=wo_planes[32 * quadrant : 32 * quadrant + 4, :, :].bitcast(I32),
-                in_=wo_scales[:, rows, :].rearrange("g r n -> r g n").bitcast(I32),
-            )
+        def load_scales(planes, scales):
+            for quadrant in range(4):
+                rows = slice(4 * quadrant, 4 * quadrant + 4)
+                nc.sync.dma_start(
+                    out=planes[32 * quadrant : 32 * quadrant + 4, :, :].bitcast(I32),
+                    in_=scales[:, rows, :].rearrange("g r n -> r g n").bitcast(I32),
+                )
+
         wo_sb = const.tile([P, E_PASSES, D * PACK], U8, align_bytes=64)
+        w1_sb = const.tile([P, F * PACK], U8, align_bytes=64)
+        load_attn(0, 4)
+        load_x(0, 2)
+        load_scales(wo_planes, wo_scales)
         for g in range(E_PASSES):
             nc.sync.dma_start(
                 out=wo_sb[:, g, :].bitcast(I32),
                 in_=wo_words[g].rearrange("p n t -> p (n t)").bitcast(I32),
             )
-        load_x(0)
-        load_attn(1)
-        for quadrant in range(4):
-            rows = slice(4 * quadrant, 4 * quadrant + 4)
-            nc.sync.dma_start(
-                out=w1_planes[32 * quadrant : 32 * quadrant + 4, :].bitcast(I32),
-                in_=w1_scales[0, rows, :].bitcast(I32),
-            )
-        w1_sb = const.tile([P, F * PACK], U8, align_bytes=64)
+        load_attn(1, 2)
+        load_x(1, 1)
+        load_x(2, 1)
+        load_attn(2, 1)
+        load_scales(w1_planes, w1_scales)
         nc.sync.dma_start(
             out=w1_sb[:].bitcast(I32), in_=w1_words[0].rearrange("p n t -> p (n t)").bitcast(I32)
         )
-        load_x(1)
-        for c in range(2, N_CHUNKS):
-            load_attn(c)
-            load_x(c)
+        for c in range(3, N_CHUNKS):
+            load_x(c, 1)
+            load_attn(c, 1)
 
         attn_t_of = {}
         attn_grouped_of = {}
@@ -165,7 +178,7 @@ def tile_tinyblock_pb_t_kernel(
 
         def add_bias(m):
             first = m * PAIR
-            xb = work.tile([P, PAIR, D], F32)
+            xb = ahead.tile([P, PAIR, D], F32)
             nc.vector.tensor_tensor(
                 out=xb[:],
                 in0=x_sb[first // CHUNK][:, first % CHUNK : first % CHUNK + PAIR, :],
@@ -264,7 +277,7 @@ def tile_tinyblock_pb_t_kernel(
                 nc.tensor.matmul_mx(
                     out=g_t_acc[:, j, :],
                     lhsT=w1_sb[:, j * P * PACK : (j + 1) * P * PACK].bitcast(FP8X4),
-                    lhsT_scale=w1_planes[:, j * P : (j + 1) * P],
+                    lhsT_scale=w1_planes[:, 0, j * P : (j + 1) * P],
                     rhs=h_codes[:].rearrange("p i r -> p (i r)").bitcast(FP8X4),
                     rhs_scale=h_scales[:].rearrange("p i r -> p (i r)"),
                     start=True,
@@ -307,19 +320,28 @@ def tile_tinyblock_pb_t_kernel(
             if 0 <= i < N_TILES and i % PAIR == PAIR - 1:
                 stage(i // PAIR)
 
-        for k in range(-5, N_TILES + 13):
+        issued = {}
+
+        def catch_up(stage, due, count, most):
+            first = issued.get(stage, 0)
+            last = min(due + 1, count, first + most)
+            for index in range(first, last):
+                stage(index)
+            issued[stage] = max(first, last)
+
+        for k in range(START, N_TILES + 16):
             run(first_matmul, k)
-            run_pair(second_matmul, k - 10)
+            run_pair(second_matmul, k - 11)
             run(normalise, k - 5)
-            run_pair(transpose_g, k - 12)
+            run_pair(transpose_g, k - 14)
             run(transpose_h, k - 7)
-            run(transpose_attn, k + 5)
-            run(regroup_attn, k + 4)
-            run_pair(gelu, k - 11)
-            run_pair(store_g, k - 13)
+            catch_up(transpose_attn, k + 5, N_TILES, 2)
+            catch_up(regroup_attn, k + 4, N_TILES, 2)
+            run_pair(gelu, k - 12)
+            run_pair(store_g, k - 15)
             run_pair(regroup_h, k - 8)
             run(mean_of_squares, k)
             run_pair(inverse_rms, k)
-            run_pair(quantise_attn, k + 3)
+            catch_up(add_bias, (k + X_LEAD) // PAIR, N_PAIRS, 1)
+            catch_up(quantise_attn, (k + 2) // PAIR, N_PAIRS, 1)
             run_pair(quantise_h, k - 9)
-            run_pair(add_bias, k + 4)

@@ -68,10 +68,17 @@ def tile_tinyblock_pb_t_kernel(
         nc.vector.memset(warm_in[:], 0.0)
         nc.scalar.activation(out=warm_out[:], in_=warm_in[:], func=ACT.Gelu)
 
-        bo_bc = const.tile([P, D], BF16)
-        nc.scalar.dma_start(out=bo_bc[:], in_=bo.partition_broadcast(P))
-        gain_bc = const.tile([P, D], BF16)
-        nc.scalar.dma_start(out=gain_bc[:], in_=mlp_norm_w.partition_broadcast(P))
+        ones = const.tile([P, P], BF16)
+        nc.vector.memset(ones[:], 1.0)
+        rows = const.tile([P, 2, D], BF16)
+        nc.vector.memset(rows[:], 0.0)
+        nc.scalar.dma_start(out=rows[0:1, 0, :], in_=bo.rearrange("(o d) -> o d", o=1))
+        nc.scalar.dma_start(out=rows[0:1, 1, :], in_=mlp_norm_w.rearrange("(o d) -> o d", o=1))
+        spread = psum_one.tile([P, 2, D], BF16, tag="spread")
+        for n in range(2):
+            nc.tensor.matmul(out=spread[:, n, :], lhsT=ones[:], rhs=rows[:, n, :], start=True, stop=True)
+        bo_bc = spread[:, 0, :]
+        gain_bc = spread[:, 1, :]
         b1_lo = const.tile([P, 1], BF16)
         nc.scalar.dma_start(out=b1_lo[:], in_=b1[0:P].rearrange("(p o) -> p o", o=1))
         b1_hi = const.tile([P, 1], BF16)
@@ -182,7 +189,7 @@ def tile_tinyblock_pb_t_kernel(
             nc.vector.tensor_tensor(
                 out=xb[:],
                 in0=x_sb[first // CHUNK][:, first % CHUNK : first % CHUNK + PAIR, :],
-                in1=bo_bc[:].unsqueeze(1).to_broadcast([P, PAIR, D]),
+                in1=bo_bc.unsqueeze(1).to_broadcast([P, PAIR, D]),
                 op=ALU.add,
             )
             xb_of[m] = xb
@@ -238,7 +245,7 @@ def tile_tinyblock_pb_t_kernel(
                 out=h[:],
                 in0=x_mid_of[i // CHUNK][:, i % CHUNK, :],
                 scalar=rstd_of[i // PAIR][:, i % PAIR : i % PAIR + 1],
-                in1=gain_bc[:],
+                in1=gain_bc,
                 op0=ALU.mult,
                 op1=ALU.mult,
             )
@@ -246,7 +253,7 @@ def tile_tinyblock_pb_t_kernel(
 
         def transpose_h(i):
             if i % PAIR == 0:
-                h_t = psum.tile([P, PAIR, 2, P], F32, tag="h_t")
+                h_t = psum_one.tile([P, PAIR, 2, P], F32, tag="h_t")
                 h_t_of[i // PAIR] = h_t
             words = h_of[i][:].bitcast(F32)
             for u in range(2):

@@ -28,6 +28,8 @@ CHUNK = 4
 N_CHUNKS = N_TILES // CHUNK
 N_PAIRS = N_TILES // PAIR
 X_LEAD = 8
+SHORT_EVERY = 99
+SHORT_LAST = 1
 START = -1
 
 FLOPS = 2 * TOKENS * (E * D + D * F)
@@ -84,6 +86,7 @@ def tile_tinyblock_pb_t_kernel(
         b1_hi = const.tile([P, 1], BF16)
         nc.scalar.dma_start(out=b1_hi[:], in_=b1[P : 2 * P].rearrange("(p o) -> p o", o=1))
         b1_half = [b1_lo, b1_hi]
+        b1_bc = const.tile([P, F], BF16)
 
         attn_sb = {}
         x_sb = {}
@@ -134,6 +137,7 @@ def tile_tinyblock_pb_t_kernel(
         nc.sync.dma_start(
             out=w1_sb[:].bitcast(I32), in_=w1_words[0].rearrange("p n t -> p (n t)").bitcast(I32)
         )
+        nc.sync.dma_start(out=b1_bc[:], in_=b1.partition_broadcast(P))
         for c in range(3, N_CHUNKS):
             load_x(c, 1)
             load_attn(c, 1)
@@ -149,10 +153,9 @@ def tile_tinyblock_pb_t_kernel(
         h_t_of = {}
         h_grouped_of = {}
         h_mx_of = {}
-        g_t_acc_of = {}
+        g_acc_of = {}
         g_t_of = {}
         g_back_of = {}
-        g_of = {}
 
         def transpose_attn(i):
             words = attn_sb[i // CHUNK][:, i % CHUNK, :].bitcast(F32)
@@ -277,30 +280,63 @@ def tile_tinyblock_pb_t_kernel(
             )
             h_mx_of[m] = (h_codes, h_scales)
 
+        def short_road(m):
+            return m % SHORT_EVERY == SHORT_EVERY - 1 or m >= N_PAIRS - SHORT_LAST
+
         def second_matmul(m):
             h_codes, h_scales = h_mx_of[m]
-            g_t_acc = psum_one.tile([P, 2, PAIR * P], F32, tag="g_t_acc")
-            for j in range(2):
-                nc.tensor.matmul_mx(
-                    out=g_t_acc[:, j, :],
-                    lhsT=w1_sb[:, j * P * PACK : (j + 1) * P * PACK].bitcast(FP8X4),
-                    lhsT_scale=w1_planes[:, 0, j * P : (j + 1) * P],
-                    rhs=h_codes[:].rearrange("p i r -> p (i r)").bitcast(FP8X4),
-                    rhs_scale=h_scales[:].rearrange("p i r -> p (i r)"),
-                    start=True,
-                    stop=True,
-                )
-            g_t_acc_of[m] = g_t_acc
+            if short_road(m):
+                g_acc = psum_one.tile([P, PAIR, F], F32, tag="g_acc")
+                for i in range(PAIR):
+                    nc.tensor.matmul_mx(
+                        out=g_acc[:, i, :],
+                        lhsT=h_codes[:, i, :].bitcast(FP8X4),
+                        lhsT_scale=h_scales[:, i, :],
+                        rhs=w1_sb[:].bitcast(FP8X4),
+                        rhs_scale=w1_planes[:, 0, :],
+                        start=True,
+                        stop=True,
+                    )
+            else:
+                g_acc = psum_one.tile([P, 2, PAIR * P], F32, tag="g_acc")
+                for j in range(2):
+                    nc.tensor.matmul_mx(
+                        out=g_acc[:, j, :],
+                        lhsT=w1_sb[:, j * P * PACK : (j + 1) * P * PACK].bitcast(FP8X4),
+                        lhsT_scale=w1_planes[:, 0, j * P : (j + 1) * P],
+                        rhs=h_codes[:].rearrange("p i r -> p (i r)").bitcast(FP8X4),
+                        rhs_scale=h_scales[:].rearrange("p i r -> p (i r)"),
+                        start=True,
+                        stop=True,
+                    )
+            g_acc_of[m] = g_acc
+
+        def store(m, g_pair):
+            nc.sync.dma_start(out=g_v[:, m * PAIR : (m + 1) * PAIR, :], in_=g_pair[:])
 
         def gelu(m):
-            g_t = work.tile([P, 2, PAIR * P], F32)
-            for j in range(2):
-                nc.scalar.activation(
-                    out=g_t[:, j, :], in_=g_t_acc_of[m][:, j, :], func=ACT.Gelu, bias=b1_half[j][:]
+            if short_road(m):
+                pre_gelu = work.tile([P, PAIR, F], F32)
+                nc.vector.tensor_tensor(
+                    out=pre_gelu[:],
+                    in0=g_acc_of[m][:],
+                    in1=b1_bc[:].unsqueeze(1).to_broadcast([P, PAIR, F]),
+                    op=ALU.add,
                 )
-            g_t_of[m] = g_t
+                g_pair = stores.tile([P, PAIR, F], F32, tag="g")
+                nc.scalar.activation(out=g_pair[:], in_=pre_gelu[:], func=ACT.Gelu)
+                store(m, g_pair)
+            else:
+                g_t = work.tile([P, 2, PAIR * P], F32)
+                for j in range(2):
+                    nc.scalar.activation(
+                        out=g_t[:, j, :], in_=g_acc_of[m][:, j, :], func=ACT.Gelu, bias=b1_half[j][:]
+                    )
+                g_t_of[m] = g_t
 
         def transpose_g(m):
+            if short_road(m):
+                return
             g_back = psum_one.tile([P, PAIR, F], F32, tag="g_back")
             for i in range(PAIR):
                 for j in range(2):
@@ -310,14 +346,11 @@ def tile_tinyblock_pb_t_kernel(
             g_back_of[m] = g_back
 
         def store_g(m):
-            first = m * PAIR
-            c = first // CHUNK
-            if first % CHUNK == 0:
-                g_c = stores.tile([P, CHUNK, F], F32, tag="g")
-                g_of[c] = g_c
-            nc.scalar.copy(out=g_of[c][:, first % CHUNK : first % CHUNK + PAIR, :], in_=g_back_of[m][:])
-            if first % CHUNK == CHUNK - PAIR:
-                nc.sync.dma_start(out=g_v[:, c * CHUNK : (c + 1) * CHUNK, :], in_=g_of[c][:])
+            if short_road(m):
+                return
+            g_pair = stores.tile([P, PAIR, F], F32, tag="g")
+            nc.scalar.copy(out=g_pair[:], in_=g_back_of[m][:])
+            store(m, g_pair)
 
         def run(stage, i):
             if 0 <= i < N_TILES:

@@ -50,7 +50,7 @@ def tile_tinyblock_pb_t_kernel(
         loads = stack.enter_context(tc.tile_pool(name="loads", bufs=N_CHUNKS))
         work = stack.enter_context(tc.tile_pool(name="work", bufs=3))
         small = stack.enter_context(tc.tile_pool(name="small", bufs=4))
-        stores = stack.enter_context(tc.tile_pool(name="stores", bufs=3))
+        stores = stack.enter_context(tc.tile_pool(name="stores", bufs=5))
         ahead = stack.enter_context(tc.tile_pool(name="ahead", bufs=X_LEAD // PAIR + 2))
         psum = stack.enter_context(tc.psum_pool(name="psum", bufs=2))
         psum_one = stack.enter_context(tc.psum_pool(name="psum_one", bufs=1))

@@ -27,7 +27,8 @@ PAIR = 2
 CHUNK = 4
 N_CHUNKS = N_TILES // CHUNK
 N_PAIRS = N_TILES // PAIR
-X_LEAD = 8
+X_LEAD = 12
+LOAD_LEAD = 16
 SHORT_EVERY = 99
 SHORT_LAST = 1
 START = -1
@@ -47,13 +48,25 @@ def tile_tinyblock_pb_t_kernel(
 
     with ExitStack() as stack:
         const = stack.enter_context(tc.tile_pool(name="const", bufs=1))
-        loads = stack.enter_context(tc.tile_pool(name="loads", bufs=N_CHUNKS))
-        work = stack.enter_context(tc.tile_pool(name="work", bufs=3))
+        loads = stack.enter_context(tc.tile_pool(name="loads", bufs=LOAD_LEAD // CHUNK + 1))
+        work = stack.enter_context(tc.tile_pool(name="work", bufs=4))
         small = stack.enter_context(tc.tile_pool(name="small", bufs=4))
-        stores = stack.enter_context(tc.tile_pool(name="stores", bufs=5))
+        stores = stack.enter_context(tc.tile_pool(name="stores", bufs=6))
         ahead = stack.enter_context(tc.tile_pool(name="ahead", bufs=X_LEAD // PAIR + 2))
         psum = stack.enter_context(tc.psum_pool(name="psum", bufs=2))
         psum_one = stack.enter_context(tc.psum_pool(name="psum_one", bufs=1))
+
+        rows = const.tile([P, 2, D], BF16)
+        nc.vector.memset(rows[:], 0.0)
+        nc.sync.dma_start(out=rows[0:1, 0, :], in_=bo.rearrange("(o d) -> o d", o=1))
+        nc.sync.dma_start(out=rows[0:1, 1, :], in_=mlp_norm_w.rearrange("(o d) -> o d", o=1))
+        ones = const.tile([P, P], BF16)
+        nc.vector.memset(ones[:], 1.0)
+        spread = psum_one.tile([P, 2, D], BF16, tag="spread")
+        for n in range(2):
+            nc.tensor.matmul(out=spread[:, n, :], lhsT=ones[:], rhs=rows[:, n, :], start=True, stop=True)
+        bo_bc = spread[:, 0, :]
+        gain_bc = spread[:, 1, :]
 
         ident = const.tile([P, P], F32)
         make_identity(nc, ident[:])
@@ -70,17 +83,6 @@ def tile_tinyblock_pb_t_kernel(
         nc.vector.memset(warm_in[:], 0.0)
         nc.scalar.activation(out=warm_out[:], in_=warm_in[:], func=ACT.Gelu)
 
-        ones = const.tile([P, P], BF16)
-        nc.vector.memset(ones[:], 1.0)
-        rows = const.tile([P, 2, D], BF16)
-        nc.vector.memset(rows[:], 0.0)
-        nc.scalar.dma_start(out=rows[0:1, 0, :], in_=bo.rearrange("(o d) -> o d", o=1))
-        nc.scalar.dma_start(out=rows[0:1, 1, :], in_=mlp_norm_w.rearrange("(o d) -> o d", o=1))
-        spread = psum_one.tile([P, 2, D], BF16, tag="spread")
-        for n in range(2):
-            nc.tensor.matmul(out=spread[:, n, :], lhsT=ones[:], rhs=rows[:, n, :], start=True, stop=True)
-        bo_bc = spread[:, 0, :]
-        gain_bc = spread[:, 1, :]
         b1_lo = const.tile([P, 1], BF16)
         nc.scalar.dma_start(out=b1_lo[:], in_=b1[0:P].rearrange("(p o) -> p o", o=1))
         b1_hi = const.tile([P, 1], BF16)
@@ -91,56 +93,59 @@ def tile_tinyblock_pb_t_kernel(
         attn_sb = {}
         x_sb = {}
 
-        def load_attn(c, pieces):
+        def new_chunk(c):
             attn_c = loads.tile([P, CHUNK, E], BF16, tag="attn")
-            tiles = CHUNK // pieces
-            for first in range(0, CHUNK, tiles):
-                nc.sync.dma_start(
-                    out=attn_c[:, first : first + tiles, :],
-                    in_=attn_v[:, c * CHUNK + first : c * CHUNK + first + tiles, :],
-                )
             attn_sb[c] = attn_c
-
-        def load_x(c, pieces):
             x_c = loads.tile([P, CHUNK, D], BF16, tag="x")
-            tiles = CHUNK // pieces
-            for first in range(0, CHUNK, tiles):
-                nc.sync.dma_start(
-                    out=x_c[:, first : first + tiles, :],
-                    in_=x_v[:, c * CHUNK + first : c * CHUNK + first + tiles, :],
-                )
             x_sb[c] = x_c
+
+        def load_chunk(c):
+            new_chunk(c)
+            load(x_sb, x_v, c * CHUNK, CHUNK)
+            load(attn_sb, attn_v, c * CHUNK, CHUNK)
+
+        for c in range(3):
+            new_chunk(c)
+
+        def load(chunks, rows_v, first, tiles):
+            at = first % CHUNK
+            nc.sync.dma_start(
+                out=chunks[first // CHUNK][:, at : at + tiles, :], in_=rows_v[:, first : first + tiles, :]
+            )
 
         def load_scales(planes, scales):
             for quadrant in range(4):
-                rows = slice(4 * quadrant, 4 * quadrant + 4)
+                four = slice(4 * quadrant, 4 * quadrant + 4)
                 nc.sync.dma_start(
                     out=planes[32 * quadrant : 32 * quadrant + 4, :, :].bitcast(I32),
-                    in_=scales[:, rows, :].rearrange("g r n -> r g n").bitcast(I32),
+                    in_=scales[:, four, :].rearrange("g r n -> r g n").bitcast(I32),
                 )
 
         wo_sb = const.tile([P, E_PASSES, D * PACK], U8, align_bytes=64)
         w1_sb = const.tile([P, F * PACK], U8, align_bytes=64)
-        load_attn(0, 4)
-        load_x(0, 2)
+        load(x_sb, x_v, 0, PAIR)
+        load(attn_sb, attn_v, 0, 1)
+        load(attn_sb, attn_v, 1, 1)
+        load(x_sb, x_v, PAIR, PAIR)
         load_scales(wo_planes, wo_scales)
         for g in range(E_PASSES):
             nc.sync.dma_start(
                 out=wo_sb[:, g, :].bitcast(I32),
                 in_=wo_words[g].rearrange("p n t -> p (n t)").bitcast(I32),
             )
-        load_attn(1, 2)
-        load_x(1, 1)
-        load_x(2, 1)
-        load_attn(2, 1)
+        load(attn_sb, attn_v, 2, 1)
+        load(attn_sb, attn_v, 3, 1)
+        load(attn_sb, attn_v, CHUNK, PAIR)
+        load(attn_sb, attn_v, CHUNK + PAIR, PAIR)
+        load(x_sb, x_v, CHUNK, CHUNK)
+        load(x_sb, x_v, 2 * CHUNK, CHUNK)
+        load(attn_sb, attn_v, 2 * CHUNK, CHUNK)
         load_scales(w1_planes, w1_scales)
         nc.sync.dma_start(
             out=w1_sb[:].bitcast(I32), in_=w1_words[0].rearrange("p n t -> p (n t)").bitcast(I32)
         )
         nc.sync.dma_start(out=b1_bc[:], in_=b1.partition_broadcast(P))
-        for c in range(3, N_CHUNKS):
-            load_x(c, 1)
-            load_attn(c, 1)
+        load_chunk(3)
 
         attn_t_of = {}
         attn_grouped_of = {}
@@ -370,6 +375,8 @@ def tile_tinyblock_pb_t_kernel(
             issued[stage] = max(first, last)
 
         for k in range(START, N_TILES + 16):
+            if (k + LOAD_LEAD) % CHUNK == 0 and 3 < (k + LOAD_LEAD) // CHUNK < N_CHUNKS:
+                load_chunk((k + LOAD_LEAD) // CHUNK)
             run(first_matmul, k)
             run_pair(second_matmul, k - 11)
             run(normalise, k - 5)

@@ -29,8 +29,10 @@ N_CHUNKS = N_TILES // CHUNK
 N_PAIRS = N_TILES // PAIR
 X_LEAD = 12
 LOAD_LEAD = 16
-SHORT_EVERY = 99
-SHORT_LAST = 1
+SINGLES = 2
+TENSOR_EVERY = 5
+SHORT_FROM = 26
+VECTOR_COPIES_FROM = 24
 START = -1
 
 FLOPS = 2 * TOKENS * (E * D + D * F)
@@ -50,6 +52,7 @@ def tile_tinyblock_pb_t_kernel(
         const = stack.enter_context(tc.tile_pool(name="const", bufs=1))
         loads = stack.enter_context(tc.tile_pool(name="loads", bufs=LOAD_LEAD // CHUNK + 1))
         work = stack.enter_context(tc.tile_pool(name="work", bufs=4))
+        grouped = stack.enter_context(tc.tile_pool(name="grouped", bufs=6))
         small = stack.enter_context(tc.tile_pool(name="small", bufs=4))
         stores = stack.enter_context(tc.tile_pool(name="stores", bufs=6))
         ahead = stack.enter_context(tc.tile_pool(name="ahead", bufs=X_LEAD // PAIR + 2))
@@ -57,19 +60,18 @@ def tile_tinyblock_pb_t_kernel(
         psum_one = stack.enter_context(tc.psum_pool(name="psum_one", bufs=1))
 
         rows = const.tile([P, 2, D], BF16)
-        nc.vector.memset(rows[:], 0.0)
-        nc.sync.dma_start(out=rows[0:1, 0, :], in_=bo.rearrange("(o d) -> o d", o=1))
-        nc.sync.dma_start(out=rows[0:1, 1, :], in_=mlp_norm_w.rearrange("(o d) -> o d", o=1))
+        for n in range(2):
+            nc.vector.memset(rows[:, n, :], 0.0)
         ones = const.tile([P, P], BF16)
         nc.vector.memset(ones[:], 1.0)
         spread = psum_one.tile([P, 2, D], BF16, tag="spread")
-        for n in range(2):
-            nc.tensor.matmul(out=spread[:, n, :], lhsT=ones[:], rhs=rows[:, n, :], start=True, stop=True)
         bo_bc = spread[:, 0, :]
         gain_bc = spread[:, 1, :]
 
         ident = const.tile([P, P], F32)
         make_identity(nc, ident[:])
+        ident_bf = const.tile([P, P], BF16)
+        nc.scalar.copy(out=ident_bf[:], in_=ident[:])
 
         wo_planes = const.tile([P, E_PASSES, D], U8, align_bytes=64)
         w1_planes = const.tile([P, 1, F], U8, align_bytes=64)
@@ -123,10 +125,14 @@ def tile_tinyblock_pb_t_kernel(
 
         wo_sb = const.tile([P, E_PASSES, D * PACK], U8, align_bytes=64)
         w1_sb = const.tile([P, F * PACK], U8, align_bytes=64)
-        load(x_sb, x_v, 0, PAIR)
         load(attn_sb, attn_v, 0, 1)
+        load(x_sb, x_v, 0, PAIR)
+        for n, row in enumerate((bo, mlp_norm_w)):
+            nc.sync.dma_start(out=rows[0:1, n, :], in_=row.rearrange("(o d) -> o d", o=1))
         load(attn_sb, attn_v, 1, 1)
         load(x_sb, x_v, PAIR, PAIR)
+        for n in range(2):
+            nc.tensor.matmul(out=spread[:, n, :], lhsT=ones[:], rhs=rows[:, n, :], start=True, stop=True)
         load_scales(wo_planes, wo_scales)
         for g in range(E_PASSES):
             nc.sync.dma_start(
@@ -174,7 +180,7 @@ def tile_tinyblock_pb_t_kernel(
 
         def regroup_attn(i):
             if i % PAIR == 0:
-                attn_grouped = work.tile([P, PAIR, E_PASSES, P, PACK], BF16, align_bytes=64)
+                attn_grouped = grouped.tile([P, PAIR, E_PASSES, P, PACK], BF16, align_bytes=64)
                 attn_grouped_of[i // PAIR] = attn_grouped
             nc.scalar.copy(
                 out=attn_grouped_of[i // PAIR][:, i % PAIR, :, :, :].bitcast(F32),
@@ -194,12 +200,25 @@ def tile_tinyblock_pb_t_kernel(
         def add_bias(m):
             first = m * PAIR
             xb = ahead.tile([P, PAIR, D], F32)
-            nc.vector.tensor_tensor(
-                out=xb[:],
-                in0=x_sb[first // CHUNK][:, first % CHUNK : first % CHUNK + PAIR, :],
-                in1=bo_bc.unsqueeze(1).to_broadcast([P, PAIR, D]),
-                op=ALU.add,
-            )
+            if m % TENSOR_EVERY == TENSOR_EVERY // 2:
+                for i in range(PAIR):
+                    x_plus_bo = psum.tile([P, D], F32, tag="acc")
+                    nc.tensor.matmul(
+                        out=x_plus_bo[:],
+                        lhsT=ident_bf[:],
+                        rhs=x_sb[first // CHUNK][:, first % CHUNK + i, :],
+                        start=True,
+                        stop=False,
+                    )
+                    nc.tensor.matmul(out=x_plus_bo[:], lhsT=ones[:], rhs=rows[:, 0, :], start=False, stop=True)
+                    nc.scalar.copy(out=xb[:, i, :], in_=x_plus_bo[:])
+            else:
+                nc.vector.tensor_tensor(
+                    out=xb[:],
+                    in0=x_sb[first // CHUNK][:, first % CHUNK : first % CHUNK + PAIR, :],
+                    in1=bo_bc.unsqueeze(1).to_broadcast([P, PAIR, D]),
+                    op=ALU.add,
+                )
             xb_of[m] = xb
 
         def first_matmul(i):
@@ -238,61 +257,81 @@ def tile_tinyblock_pb_t_kernel(
                 accum_out=mean_sq_of[i // PAIR][:, i % PAIR : i % PAIR + 1],
             )
 
-        def inverse_rms(m):
+        def how_many(first):
+            return 1 if first >= N_TILES - SINGLES else PAIR
+
+        def inverse_rms(first):
+            some = slice(first % PAIR, first % PAIR + how_many(first))
             mean_sq_eps = small.tile([P, PAIR], F32)
             nc.gpsimd.tensor_scalar(
-                out=mean_sq_eps[:], in0=mean_sq_of[m][:], scalar1=1.0, scalar2=EPS, op0=ALU.mult, op1=ALU.add
+                out=mean_sq_eps[:, some],
+                in0=mean_sq_of[first // PAIR][:, some],
+                scalar1=1.0,
+                scalar2=EPS,
+                op0=ALU.mult,
+                op1=ALU.add,
             )
             rstd = small.tile([P, PAIR], F32)
-            nc.gpsimd.tensor_tensor(out=rstd[:], in0=mean_sq_eps[:], in1=neg_half[:], op=ALU.pow)
-            rstd_of[m] = rstd
+            nc.gpsimd.tensor_tensor(
+                out=rstd[:, some], in0=mean_sq_eps[:, some], in1=neg_half[:, some], op=ALU.pow
+            )
+            for i in range(first, first + how_many(first)):
+                rstd_of[i] = rstd[:, i % PAIR : i % PAIR + 1]
 
         def normalise(i):
             h = work.tile([P, D], BF16)
             nc.vector.scalar_tensor_tensor(
                 out=h[:],
                 in0=x_mid_of[i // CHUNK][:, i % CHUNK, :],
-                scalar=rstd_of[i // PAIR][:, i % PAIR : i % PAIR + 1],
+                scalar=rstd_of[i],
                 in1=gain_bc,
                 op0=ALU.mult,
                 op1=ALU.mult,
             )
             h_of[i] = h
 
-        def transpose_h(i):
-            if i % PAIR == 0:
+        def transpose_h(first):
+            tiles = how_many(first)
+            if tiles == 1:
+                h_t = psum.tile([P, 1, 2, P], F32, tag="attn_t")
+            else:
                 h_t = psum_one.tile([P, PAIR, 2, P], F32, tag="h_t")
-                h_t_of[i // PAIR] = h_t
-            words = h_of[i][:].bitcast(F32)
-            for u in range(2):
-                nc.tensor.transpose(h_t_of[i // PAIR][:, i % PAIR, u, :], words[:, u::2], ident[:])
+            for i in range(tiles):
+                words = h_of[first + i][:].bitcast(F32)
+                for u in range(2):
+                    nc.tensor.transpose(h_t[:, i, u, :], words[:, u::2], ident[:])
+            h_t_of[first] = h_t
 
-        def regroup_h(m):
-            h_grouped = work.tile([P, PAIR, P, PACK], BF16, align_bytes=64)
+        def regroup_h(first):
+            h_grouped = work.tile([P, how_many(first), P, PACK], BF16, tag="h_grouped", align_bytes=64)
             nc.scalar.copy(
                 out=h_grouped[:].bitcast(F32),
-                in_=h_t_of[m][:].rearrange("p i u r -> p i r u"),
+                in_=h_t_of[first][:].rearrange("p i u r -> p i r u"),
             )
-            h_grouped_of[m] = h_grouped
+            h_grouped_of[first] = h_grouped
 
-        def quantise_h(m):
-            h_codes = work.tile([P, PAIR, P], U32, align_bytes=64)
-            h_scales = work.tile([P, PAIR, P], U8, align_bytes=64)
+        def quantise_h(first):
+            h_codes = work.tile([P, how_many(first), P], U32, tag="h_codes", align_bytes=64)
+            h_scales = work.tile([P, how_many(first), P], U8, tag="h_scales", align_bytes=64)
             nc.vector.quantize_mx(
                 out=h_codes[:].rearrange("p i r -> p (i r)").bitcast(FP8X4),
                 scales=h_scales[:].rearrange("p i r -> p (i r)"),
-                in_=h_grouped_of[m][:].rearrange("p i r t -> p (i r t)"),
+                in_=h_grouped_of[first][:].rearrange("p i r t -> p (i r t)"),
             )
-            h_mx_of[m] = (h_codes, h_scales)
+            h_mx_of[first] = (h_codes, h_scales)
 
-        def short_road(m):
-            return m % SHORT_EVERY == SHORT_EVERY - 1 or m >= N_PAIRS - SHORT_LAST
+        def short_road(first):
+            return first >= SHORT_FROM
 
-        def second_matmul(m):
-            h_codes, h_scales = h_mx_of[m]
-            if short_road(m):
-                g_acc = psum_one.tile([P, PAIR, F], F32, tag="g_acc")
-                for i in range(PAIR):
+        def second_matmul(first):
+            h_codes, h_scales = h_mx_of[first]
+            tiles = how_many(first)
+            if short_road(first):
+                if tiles == 1:
+                    g_acc = psum.tile([P, 1, F], F32, tag="acc")
+                else:
+                    g_acc = psum_one.tile([P, PAIR, F], F32, tag="g_acc")
+                for i in range(tiles):
                     nc.tensor.matmul_mx(
                         out=g_acc[:, i, :],
                         lhsT=h_codes[:, i, :].bitcast(FP8X4),
@@ -314,56 +353,62 @@ def tile_tinyblock_pb_t_kernel(
                         start=True,
                         stop=True,
                     )
-            g_acc_of[m] = g_acc
+            g_acc_of[first] = g_acc
 
-        def store(m, g_pair):
-            nc.sync.dma_start(out=g_v[:, m * PAIR : (m + 1) * PAIR, :], in_=g_pair[:])
+        def store(first, g_out):
+            nc.sync.dma_start(out=g_v[:, first : first + how_many(first), :], in_=g_out[:])
 
-        def gelu(m):
-            if short_road(m):
-                pre_gelu = work.tile([P, PAIR, F], F32)
+        def gelu(first):
+            tiles = how_many(first)
+            if short_road(first):
+                pre_gelu = work.tile([P, tiles, F], F32, tag="pre_gelu")
                 nc.vector.tensor_tensor(
                     out=pre_gelu[:],
-                    in0=g_acc_of[m][:],
-                    in1=b1_bc[:].unsqueeze(1).to_broadcast([P, PAIR, F]),
+                    in0=g_acc_of[first][:],
+                    in1=b1_bc[:].unsqueeze(1).to_broadcast([P, tiles, F]),
                     op=ALU.add,
                 )
-                g_pair = stores.tile([P, PAIR, F], F32, tag="g")
-                nc.scalar.activation(out=g_pair[:], in_=pre_gelu[:], func=ACT.Gelu)
-                store(m, g_pair)
+                g_out = stores.tile([P, tiles, F], F32, tag="g")
+                nc.scalar.activation(out=g_out[:], in_=pre_gelu[:], func=ACT.Gelu)
+                store(first, g_out)
             else:
                 g_t = work.tile([P, 2, PAIR * P], F32)
                 for j in range(2):
                     nc.scalar.activation(
-                        out=g_t[:, j, :], in_=g_acc_of[m][:, j, :], func=ACT.Gelu, bias=b1_half[j][:]
+                        out=g_t[:, j, :], in_=g_acc_of[first][:, j, :], func=ACT.Gelu, bias=b1_half[j][:]
                     )
-                g_t_of[m] = g_t
+                g_t_of[first] = g_t
 
-        def transpose_g(m):
-            if short_road(m):
+        def transpose_g(first):
+            if short_road(first):
                 return
             g_back = psum_one.tile([P, PAIR, F], F32, tag="g_back")
             for i in range(PAIR):
                 for j in range(2):
                     nc.tensor.transpose(
-                        g_back[:, i, j * P : (j + 1) * P], g_t_of[m][:, j, i * P : (i + 1) * P], ident[:]
+                        g_back[:, i, j * P : (j + 1) * P], g_t_of[first][:, j, i * P : (i + 1) * P], ident[:]
                     )
-            g_back_of[m] = g_back
+            g_back_of[first] = g_back
 
-        def store_g(m):
-            if short_road(m):
+        def store_g(first):
+            if short_road(first):
                 return
-            g_pair = stores.tile([P, PAIR, F], F32, tag="g")
-            nc.scalar.copy(out=g_pair[:], in_=g_back_of[m][:])
-            store(m, g_pair)
+            g_out = stores.tile([P, PAIR, F], F32, tag="g")
+            if first >= VECTOR_COPIES_FROM:
+                nc.vector.tensor_copy(out=g_out[:], in_=g_back_of[first][:])
+            else:
+                nc.scalar.copy(out=g_out[:], in_=g_back_of[first][:])
+            store(first, g_out)
 
         def run(stage, i):
             if 0 <= i < N_TILES:
                 stage(i)
 
-        def run_pair(stage, i):
-            if 0 <= i < N_TILES and i % PAIR == PAIR - 1:
-                stage(i // PAIR)
+        def run_group(stage, i):
+            if N_TILES - SINGLES <= i < N_TILES:
+                stage(i)
+            elif 0 <= i < N_TILES and i % PAIR == PAIR - 1:
+                stage(i - PAIR + 1)
 
         issued = {}
 
@@ -374,21 +419,21 @@ def tile_tinyblock_pb_t_kernel(
                 stage(index)
             issued[stage] = max(first, last)
 
-        for k in range(START, N_TILES + 16):
+        for k in range(START, N_TILES + 12):
             if (k + LOAD_LEAD) % CHUNK == 0 and 3 < (k + LOAD_LEAD) // CHUNK < N_CHUNKS:
                 load_chunk((k + LOAD_LEAD) // CHUNK)
             run(first_matmul, k)
-            run_pair(second_matmul, k - 11)
-            run(normalise, k - 5)
-            run_pair(transpose_g, k - 14)
-            run(transpose_h, k - 7)
-            catch_up(transpose_attn, k + 5, N_TILES, 2)
-            catch_up(regroup_attn, k + 4, N_TILES, 2)
-            run_pair(gelu, k - 12)
-            run_pair(store_g, k - 15)
-            run_pair(regroup_h, k - 8)
+            run_group(second_matmul, k - 8)
+            run(normalise, k - 4)
+            run_group(transpose_g, k - 10)
+            run_group(transpose_h, k - 5)
+            catch_up(transpose_attn, k + 9, N_TILES, 2)
+            catch_up(regroup_attn, k + 8, N_TILES, 2)
+            run_group(gelu, k - 9)
+            run_group(store_g, k - 11)
+            run_group(regroup_h, k - 6)
             run(mean_of_squares, k)
-            run_pair(inverse_rms, k)
+            run_group(inverse_rms, k)
             catch_up(add_bias, (k + X_LEAD) // PAIR, N_PAIRS, 1)
             catch_up(quantise_attn, (k + 2) // PAIR, N_PAIRS, 1)
-            run_pair(quantise_h, k - 9)
+            run_group(quantise_h, k - 7)

@@ -61,7 +61,7 @@ def tile_tinyblock_pb_t_kernel(
 
         rows = const.tile([P, 2, D], BF16)
         for n in range(2):
-            nc.vector.memset(rows[:, n, :], 0.0)
+            nc.vector.memset(rows[:, n, :].bitcast(I32), 0)
         ones = const.tile([P, P], BF16)
         nc.vector.memset(ones[:], 1.0)
         spread = psum_one.tile([P, 2, D], BF16, tag="spread")
@@ -126,11 +126,12 @@ def tile_tinyblock_pb_t_kernel(
         wo_sb = const.tile([P, E_PASSES, D * PACK], U8, align_bytes=64)
         w1_sb = const.tile([P, F * PACK], U8, align_bytes=64)
         load(attn_sb, attn_v, 0, 1)
-        load(x_sb, x_v, 0, PAIR)
         for n, row in enumerate((bo, mlp_norm_w)):
             nc.sync.dma_start(out=rows[0:1, n, :], in_=row.rearrange("(o d) -> o d", o=1))
+        load(x_sb, x_v, 0, PAIR)
         load(attn_sb, attn_v, 1, 1)
         load(x_sb, x_v, PAIR, PAIR)
+        load(attn_sb, attn_v, 2, 1)
         for n in range(2):
             nc.tensor.matmul(out=spread[:, n, :], lhsT=ones[:], rhs=rows[:, n, :], start=True, stop=True)
         load_scales(wo_planes, wo_scales)
@@ -139,11 +140,10 @@ def tile_tinyblock_pb_t_kernel(
                 out=wo_sb[:, g, :].bitcast(I32),
                 in_=wo_words[g].rearrange("p n t -> p (n t)").bitcast(I32),
             )
-        load(attn_sb, attn_v, 2, 1)
+        load(x_sb, x_v, CHUNK, CHUNK)
         load(attn_sb, attn_v, 3, 1)
         load(attn_sb, attn_v, CHUNK, PAIR)
         load(attn_sb, attn_v, CHUNK + PAIR, PAIR)
-        load(x_sb, x_v, CHUNK, CHUNK)
         load(x_sb, x_v, 2 * CHUNK, CHUNK)
         load(attn_sb, attn_v, 2 * CHUNK, CHUNK)
         load_scales(w1_planes, w1_scales)

@@ -27,9 +27,10 @@ PAIR = 2
 CHUNK = 4
 N_CHUNKS = N_TILES // CHUNK
 N_PAIRS = N_TILES // PAIR
-X_LEAD = 12
+X_LEAD = 8
 LOAD_LEAD = 16
 SINGLES = 2
+PAD = 8
 TENSOR_EVERY = 5
 SHORT_FROM = 26
 VECTOR_COPIES_FROM = 24
@@ -236,22 +237,23 @@ def tile_tinyblock_pb_t_kernel(
                 )
             c = i // CHUNK
             if i % CHUNK == 0:
-                x_mid_c = stores.tile([P, CHUNK, D], F32, tag="x_mid")
+                x_mid_c = stores.tile([P, CHUNK, D + PAD], F32, tag="x_mid")
+                nc.gpsimd.memset(x_mid_c[:, :, D : D + 1], math.sqrt(EPS * D))
                 x_mid_of[c] = x_mid_c
             nc.vector.tensor_tensor(
-                out=x_mid_of[c][:, i % CHUNK, :], in0=acc[:], in1=xb_of[i // PAIR][:, i % PAIR, :], op=ALU.add
+                out=x_mid_of[c][:, i % CHUNK, :D], in0=acc[:], in1=xb_of[i // PAIR][:, i % PAIR, :], op=ALU.add
             )
             if i % CHUNK == CHUNK - 1:
-                nc.sync.dma_start(out=x_mid_v[:, c * CHUNK : (c + 1) * CHUNK, :], in_=x_mid_of[c][:])
+                nc.sync.dma_start(out=x_mid_v[:, c * CHUNK : (c + 1) * CHUNK, :], in_=x_mid_of[c][:, :, :D])
 
         def mean_of_squares(i):
             if i % PAIR == 0:
                 mean_sq = small.tile([P, PAIR], F32)
                 mean_sq_of[i // PAIR] = mean_sq
-            squares = work.tile([P, D], BF16)
+            squares = work.tile([P, D + 1], BF16)
             nc.scalar.activation(
                 out=squares[:],
-                in_=x_mid_of[i // CHUNK][:, i % CHUNK, :],
+                in_=x_mid_of[i // CHUNK][:, i % CHUNK, : D + 1],
                 func=ACT.Square,
                 scale=1.0 / math.sqrt(D),
                 accum_out=mean_sq_of[i // PAIR][:, i % PAIR : i % PAIR + 1],
@@ -262,18 +264,9 @@ def tile_tinyblock_pb_t_kernel(
 
         def inverse_rms(first):
             some = slice(first % PAIR, first % PAIR + how_many(first))
-            mean_sq_eps = small.tile([P, PAIR], F32)
-            nc.gpsimd.tensor_scalar(
-                out=mean_sq_eps[:, some],
-                in0=mean_sq_of[first // PAIR][:, some],
-                scalar1=1.0,
-                scalar2=EPS,
-                op0=ALU.mult,
-                op1=ALU.add,
-            )
             rstd = small.tile([P, PAIR], F32)
             nc.gpsimd.tensor_tensor(
-                out=rstd[:, some], in0=mean_sq_eps[:, some], in1=neg_half[:, some], op=ALU.pow
+                out=rstd[:, some], in0=mean_sq_of[first // PAIR][:, some], in1=neg_half[:, some], op=ALU.pow
             )
             for i in range(first, first + how_many(first)):
                 rstd_of[i] = rstd[:, i % PAIR : i % PAIR + 1]
@@ -282,7 +275,7 @@ def tile_tinyblock_pb_t_kernel(
             h = work.tile([P, D], BF16)
             nc.vector.scalar_tensor_tensor(
                 out=h[:],
-                in0=x_mid_of[i // CHUNK][:, i % CHUNK, :],
+                in0=x_mid_of[i // CHUNK][:, i % CHUNK, :D],
                 scalar=rstd_of[i],
                 in1=gain_bc,
                 op0=ALU.mult,

import math
from contextlib import ExitStack

import concourse.mybir as mybir
from concourse.masks import make_identity

F32 = mybir.dt.float32
BF16 = mybir.dt.bfloat16
I32 = mybir.dt.int32
U32 = mybir.dt.uint32
U8 = mybir.dt.uint8
FP8X4 = mybir.dt.float8_e4m3fn_x4
ACT = mybir.ActivationFunctionType
ALU = mybir.AluOpType

P = 128
PACK = 4
K_PASS = P * PACK
TOKENS = 4 * 1024
E = 1024
D = 512
F = 256
EPS = 1e-6
E_PASSES = E // K_PASS
N_TILES = TOKENS // P
PAIR = 2
CHUNK = 4
N_CHUNKS = N_TILES // CHUNK
N_PAIRS = N_TILES // PAIR
X_LEAD = 8
LOAD_LEAD = 16
SINGLES = 2
PAD = 8
TENSOR_EVERY = 5
SHORT_FROM = 26
VECTOR_COPIES_FROM = 24
START = -1

FLOPS = 2 * TOKENS * (E * D + D * F)


def tile_tinyblock_pb_t_kernel(
    tc, attn, x, wo_words, wo_scales, bo, mlp_norm_w, w1_words, w1_scales, b1, out_0, out_1
):
    nc = tc.nc

    attn_v = attn.flatten_outer_dims().rearrange("(p i) k -> p i k", i=N_TILES)
    x_v = x.flatten_outer_dims().rearrange("(p i) d -> p i d", i=N_TILES)
    x_mid_v = out_0.flatten_outer_dims().rearrange("(p i) d -> p i d", i=N_TILES)
    g_v = out_1.flatten_outer_dims().rearrange("(p i) f -> p i f", i=N_TILES)

    with ExitStack() as stack:
        const = stack.enter_context(tc.tile_pool(name="const", bufs=1))
        loads = stack.enter_context(tc.tile_pool(name="loads", bufs=LOAD_LEAD // CHUNK + 1))
        work = stack.enter_context(tc.tile_pool(name="work", bufs=4))
        grouped = stack.enter_context(tc.tile_pool(name="grouped", bufs=6))
        small = stack.enter_context(tc.tile_pool(name="small", bufs=4))
        stores = stack.enter_context(tc.tile_pool(name="stores", bufs=6))
        ahead = stack.enter_context(tc.tile_pool(name="ahead", bufs=X_LEAD // PAIR + 2))
        psum = stack.enter_context(tc.psum_pool(name="psum", bufs=2))
        psum_one = stack.enter_context(tc.psum_pool(name="psum_one", bufs=1))

        rows = const.tile([P, 2, D], BF16)
        for n in range(2):
            nc.vector.memset(rows[:, n, :].bitcast(I32), 0)
        ones = const.tile([P, P], BF16)
        nc.vector.memset(ones[:], 1.0)
        spread = psum_one.tile([P, 2, D], BF16, tag="spread")
        bo_bc = spread[:, 0, :]
        gain_bc = spread[:, 1, :]

        ident = const.tile([P, P], F32)
        make_identity(nc, ident[:])
        ident_bf = const.tile([P, P], BF16)
        nc.scalar.copy(out=ident_bf[:], in_=ident[:])

        wo_planes = const.tile([P, E_PASSES, D], U8, align_bytes=64)
        w1_planes = const.tile([P, 1, F], U8, align_bytes=64)
        nc.vector.memset(wo_planes[:].bitcast(I32), 0)
        nc.vector.memset(w1_planes[:].bitcast(I32), 0)
        neg_half = const.tile([P, PAIR], F32)
        nc.vector.memset(neg_half[:], -0.5)

        warm_in = const.tile([P, 1], F32)
        warm_out = const.tile([P, 1], F32)
        nc.vector.memset(warm_in[:], 0.0)
        nc.scalar.activation(out=warm_out[:], in_=warm_in[:], func=ACT.Gelu)

        b1_lo = const.tile([P, 1], BF16)
        nc.scalar.dma_start(out=b1_lo[:], in_=b1[0:P].rearrange("(p o) -> p o", o=1))
        b1_hi = const.tile([P, 1], BF16)
        nc.scalar.dma_start(out=b1_hi[:], in_=b1[P : 2 * P].rearrange("(p o) -> p o", o=1))
        b1_half = [b1_lo, b1_hi]
        b1_bc = const.tile([P, F], BF16)

        attn_sb = {}
        x_sb = {}

        def new_chunk(c):
            attn_c = loads.tile([P, CHUNK, E], BF16, tag="attn")
            attn_sb[c] = attn_c
            x_c = loads.tile([P, CHUNK, D], BF16, tag="x")
            x_sb[c] = x_c

        def load_chunk(c):
            new_chunk(c)
            load(x_sb, x_v, c * CHUNK, CHUNK)
            load(attn_sb, attn_v, c * CHUNK, CHUNK)

        for c in range(3):
            new_chunk(c)

        def load(chunks, rows_v, first, tiles):
            at = first % CHUNK
            nc.sync.dma_start(
                out=chunks[first // CHUNK][:, at : at + tiles, :], in_=rows_v[:, first : first + tiles, :]
            )

        def load_scales(planes, scales):
            for quadrant in range(4):
                four = slice(4 * quadrant, 4 * quadrant + 4)
                nc.sync.dma_start(
                    out=planes[32 * quadrant : 32 * quadrant + 4, :, :].bitcast(I32),
                    in_=scales[:, four, :].rearrange("g r n -> r g n").bitcast(I32),
                )

        wo_sb = const.tile([P, E_PASSES, D * PACK], U8, align_bytes=64)
        w1_sb = const.tile([P, F * PACK], U8, align_bytes=64)
        load(attn_sb, attn_v, 0, 1)
        for n, row in enumerate((bo, mlp_norm_w)):
            nc.sync.dma_start(out=rows[0:1, n, :], in_=row.rearrange("(o d) -> o d", o=1))
        load(x_sb, x_v, 0, PAIR)
        load(attn_sb, attn_v, 1, 1)
        load(x_sb, x_v, PAIR, PAIR)
        load(attn_sb, attn_v, 2, 1)
        for n in range(2):
            nc.tensor.matmul(out=spread[:, n, :], lhsT=ones[:], rhs=rows[:, n, :], start=True, stop=True)
        load_scales(wo_planes, wo_scales)
        for g in range(E_PASSES):
            nc.sync.dma_start(
                out=wo_sb[:, g, :].bitcast(I32),
                in_=wo_words[g].rearrange("p n t -> p (n t)").bitcast(I32),
            )
        load(x_sb, x_v, CHUNK, CHUNK)
        load(attn_sb, attn_v, 3, 1)
        load(attn_sb, attn_v, CHUNK, PAIR)
        load(attn_sb, attn_v, CHUNK + PAIR, PAIR)
        load(x_sb, x_v, 2 * CHUNK, CHUNK)
        load(attn_sb, attn_v, 2 * CHUNK, CHUNK)
        load_scales(w1_planes, w1_scales)
        nc.sync.dma_start(
            out=w1_sb[:].bitcast(I32), in_=w1_words[0].rearrange("p n t -> p (n t)").bitcast(I32)
        )
        nc.sync.dma_start(out=b1_bc[:], in_=b1.partition_broadcast(P))
        load_chunk(3)

        attn_t_of = {}
        attn_grouped_of = {}
        attn_mx_of = {}
        xb_of = {}
        x_mid_of = {}
        mean_sq_of = {}
        rstd_of = {}
        h_of = {}
        h_t_of = {}
        h_grouped_of = {}
        h_mx_of = {}
        g_acc_of = {}
        g_t_of = {}
        g_back_of = {}

        def transpose_attn(i):
            words = attn_sb[i // CHUNK][:, i % CHUNK, :].bitcast(F32)
            attn_t = psum.tile([P, E_PASSES, 2, P], F32, tag="attn_t")
            for g in range(E_PASSES):
                for u in range(2):
                    nc.tensor.transpose(
                        attn_t[:, g, u, :], words[:, 256 * g + u : 256 * (g + 1) : 2], ident[:]
                    )
            attn_t_of[i] = attn_t

        def regroup_attn(i):
            if i % PAIR == 0:
                attn_grouped = grouped.tile([P, PAIR, E_PASSES, P, PACK], BF16, align_bytes=64)
                attn_grouped_of[i // PAIR] = attn_grouped
            nc.scalar.copy(
                out=attn_grouped_of[i // PAIR][:, i % PAIR, :, :, :].bitcast(F32),
                in_=attn_t_of[i][:].rearrange("p g u r -> p g r u"),
            )

        def quantise_attn(m):
            attn_codes = work.tile([P, PAIR, E_PASSES, P], U32, align_bytes=64)
            attn_scales = work.tile([P, PAIR, E_PASSES, P], U8, align_bytes=64)
            nc.vector.quantize_mx(
                out=attn_codes[:].rearrange("p i g r -> p (i g r)").bitcast(FP8X4),
                scales=attn_scales[:].rearrange("p i g r -> p (i g r)"),
                in_=attn_grouped_of[m][:].rearrange("p i g r t -> p (i g r t)"),
            )
            attn_mx_of[m] = (attn_codes, attn_scales)

        def add_bias(m):
            first = m * PAIR
            xb = ahead.tile([P, PAIR, D], F32)
            if m % TENSOR_EVERY == TENSOR_EVERY // 2:
                for i in range(PAIR):
                    x_plus_bo = psum.tile([P, D], F32, tag="acc")
                    nc.tensor.matmul(
                        out=x_plus_bo[:],
                        lhsT=ident_bf[:],
                        rhs=x_sb[first // CHUNK][:, first % CHUNK + i, :],
                        start=True,
                        stop=False,
                    )
                    nc.tensor.matmul(out=x_plus_bo[:], lhsT=ones[:], rhs=rows[:, 0, :], start=False, stop=True)
                    nc.scalar.copy(out=xb[:, i, :], in_=x_plus_bo[:])
            else:
                nc.vector.tensor_tensor(
                    out=xb[:],
                    in0=x_sb[first // CHUNK][:, first % CHUNK : first % CHUNK + PAIR, :],
                    in1=bo_bc.unsqueeze(1).to_broadcast([P, PAIR, D]),
                    op=ALU.add,
                )
            xb_of[m] = xb

        def first_matmul(i):
            attn_codes, attn_scales = attn_mx_of[i // PAIR]
            acc = psum.tile([P, D], F32, tag="acc")
            for g in range(E_PASSES):
                nc.tensor.matmul_mx(
                    out=acc[:],
                    lhsT=attn_codes[:, i % PAIR, g, :].bitcast(FP8X4),
                    lhsT_scale=attn_scales[:, i % PAIR, g, :],
                    rhs=wo_sb[:, g, :].bitcast(FP8X4),
                    rhs_scale=wo_planes[:, g, :],
                    start=(g == 0),
                    stop=(g == E_PASSES - 1),
                )
            c = i // CHUNK
            if i % CHUNK == 0:
                x_mid_c = stores.tile([P, CHUNK, D + PAD], F32, tag="x_mid")
                nc.gpsimd.memset(x_mid_c[:, :, D : D + 1], math.sqrt(EPS * D))
                x_mid_of[c] = x_mid_c
            nc.vector.tensor_tensor(
                out=x_mid_of[c][:, i % CHUNK, :D], in0=acc[:], in1=xb_of[i // PAIR][:, i % PAIR, :], op=ALU.add
            )
            if i % CHUNK == CHUNK - 1:
                nc.sync.dma_start(out=x_mid_v[:, c * CHUNK : (c + 1) * CHUNK, :], in_=x_mid_of[c][:, :, :D])

        def mean_of_squares(i):
            if i % PAIR == 0:
                mean_sq = small.tile([P, PAIR], F32)
                mean_sq_of[i // PAIR] = mean_sq
            squares = work.tile([P, D + 1], BF16)
            nc.scalar.activation(
                out=squares[:],
                in_=x_mid_of[i // CHUNK][:, i % CHUNK, : D + 1],
                func=ACT.Square,
                scale=1.0 / math.sqrt(D),
                accum_out=mean_sq_of[i // PAIR][:, i % PAIR : i % PAIR + 1],
            )

        def how_many(first):
            return 1 if first >= N_TILES - SINGLES else PAIR

        def inverse_rms(first):
            some = slice(first % PAIR, first % PAIR + how_many(first))
            rstd = small.tile([P, PAIR], F32)
            nc.gpsimd.tensor_tensor(
                out=rstd[:, some], in0=mean_sq_of[first // PAIR][:, some], in1=neg_half[:, some], op=ALU.pow
            )
            for i in range(first, first + how_many(first)):
                rstd_of[i] = rstd[:, i % PAIR : i % PAIR + 1]

        def normalise(i):
            h = work.tile([P, D], BF16)
            nc.vector.scalar_tensor_tensor(
                out=h[:],
                in0=x_mid_of[i // CHUNK][:, i % CHUNK, :D],
                scalar=rstd_of[i],
                in1=gain_bc,
                op0=ALU.mult,
                op1=ALU.mult,
            )
            h_of[i] = h

        def transpose_h(first):
            tiles = how_many(first)
            if tiles == 1:
                h_t = psum.tile([P, 1, 2, P], F32, tag="attn_t")
            else:
                h_t = psum_one.tile([P, PAIR, 2, P], F32, tag="h_t")
            for i in range(tiles):
                words = h_of[first + i][:].bitcast(F32)
                for u in range(2):
                    nc.tensor.transpose(h_t[:, i, u, :], words[:, u::2], ident[:])
            h_t_of[first] = h_t

        def regroup_h(first):
            h_grouped = work.tile([P, how_many(first), P, PACK], BF16, tag="h_grouped", align_bytes=64)
            nc.scalar.copy(
                out=h_grouped[:].bitcast(F32),
                in_=h_t_of[first][:].rearrange("p i u r -> p i r u"),
            )
            h_grouped_of[first] = h_grouped

        def quantise_h(first):
            h_codes = work.tile([P, how_many(first), P], U32, tag="h_codes", align_bytes=64)
            h_scales = work.tile([P, how_many(first), P], U8, tag="h_scales", align_bytes=64)
            nc.vector.quantize_mx(
                out=h_codes[:].rearrange("p i r -> p (i r)").bitcast(FP8X4),
                scales=h_scales[:].rearrange("p i r -> p (i r)"),
                in_=h_grouped_of[first][:].rearrange("p i r t -> p (i r t)"),
            )
            h_mx_of[first] = (h_codes, h_scales)

        def short_road(first):
            return first >= SHORT_FROM

        def second_matmul(first):
            h_codes, h_scales = h_mx_of[first]
            tiles = how_many(first)
            if short_road(first):
                if tiles == 1:
                    g_acc = psum.tile([P, 1, F], F32, tag="acc")
                else:
                    g_acc = psum_one.tile([P, PAIR, F], F32, tag="g_acc")
                for i in range(tiles):
                    nc.tensor.matmul_mx(
                        out=g_acc[:, i, :],
                        lhsT=h_codes[:, i, :].bitcast(FP8X4),
                        lhsT_scale=h_scales[:, i, :],
                        rhs=w1_sb[:].bitcast(FP8X4),
                        rhs_scale=w1_planes[:, 0, :],
                        start=True,
                        stop=True,
                    )
            else:
                g_acc = psum_one.tile([P, 2, PAIR * P], F32, tag="g_acc")
                for j in range(2):
                    nc.tensor.matmul_mx(
                        out=g_acc[:, j, :],
                        lhsT=w1_sb[:, j * P * PACK : (j + 1) * P * PACK].bitcast(FP8X4),
                        lhsT_scale=w1_planes[:, 0, j * P : (j + 1) * P],
                        rhs=h_codes[:].rearrange("p i r -> p (i r)").bitcast(FP8X4),
                        rhs_scale=h_scales[:].rearrange("p i r -> p (i r)"),
                        start=True,
                        stop=True,
                    )
            g_acc_of[first] = g_acc

        def store(first, g_out):
            nc.sync.dma_start(out=g_v[:, first : first + how_many(first), :], in_=g_out[:])

        def gelu(first):
            tiles = how_many(first)
            if short_road(first):
                pre_gelu = work.tile([P, tiles, F], F32, tag="pre_gelu")
                nc.vector.tensor_tensor(
                    out=pre_gelu[:],
                    in0=g_acc_of[first][:],
                    in1=b1_bc[:].unsqueeze(1).to_broadcast([P, tiles, F]),
                    op=ALU.add,
                )
                g_out = stores.tile([P, tiles, F], F32, tag="g")
                nc.scalar.activation(out=g_out[:], in_=pre_gelu[:], func=ACT.Gelu)
                store(first, g_out)
            else:
                g_t = work.tile([P, 2, PAIR * P], F32)
                for j in range(2):
                    nc.scalar.activation(
                        out=g_t[:, j, :], in_=g_acc_of[first][:, j, :], func=ACT.Gelu, bias=b1_half[j][:]
                    )
                g_t_of[first] = g_t

        def transpose_g(first):
            if short_road(first):
                return
            g_back = psum_one.tile([P, PAIR, F], F32, tag="g_back")
            for i in range(PAIR):
                for j in range(2):
                    nc.tensor.transpose(
                        g_back[:, i, j * P : (j + 1) * P], g_t_of[first][:, j, i * P : (i + 1) * P], ident[:]
                    )
            g_back_of[first] = g_back

        def store_g(first):
            if short_road(first):
                return
            g_out = stores.tile([P, PAIR, F], F32, tag="g")
            if first >= VECTOR_COPIES_FROM:
                nc.vector.tensor_copy(out=g_out[:], in_=g_back_of[first][:])
            else:
                nc.scalar.copy(out=g_out[:], in_=g_back_of[first][:])
            store(first, g_out)

        def run(stage, i):
            if 0 <= i < N_TILES:
                stage(i)

        def run_group(stage, i):
            if N_TILES - SINGLES <= i < N_TILES:
                stage(i)
            elif 0 <= i < N_TILES and i % PAIR == PAIR - 1:
                stage(i - PAIR + 1)

        issued = {}

        def catch_up(stage, due, count, most):
            first = issued.get(stage, 0)
            last = min(due + 1, count, first + most)
            for index in range(first, last):
                stage(index)
            issued[stage] = max(first, last)

        for k in range(START, N_TILES + 12):
            if (k + LOAD_LEAD) % CHUNK == 0 and 3 < (k + LOAD_LEAD) // CHUNK < N_CHUNKS:
                load_chunk((k + LOAD_LEAD) // CHUNK)
            run(first_matmul, k)
            run_group(second_matmul, k - 8)
            run(normalise, k - 4)
            run_group(transpose_g, k - 10)
            run_group(transpose_h, k - 5)
            catch_up(transpose_attn, k + 9, N_TILES, 2)
            catch_up(regroup_attn, k + 8, N_TILES, 2)
            run_group(gelu, k - 9)
            run_group(store_g, k - 11)
            run_group(regroup_h, k - 6)
            run(mean_of_squares, k)
            run_group(inverse_rms, k)
            catch_up(add_bias, (k + X_LEAD) // PAIR, N_PAIRS, 1)
            catch_up(quantise_attn, (k + 2) // PAIR, N_PAIRS, 1)
            run_group(quantise_h, k - 7)
